import numpy as np
import ml_dtypes


def mxq(x, axis, fmt="e4m3"):
    dtype, down = {"e4m3": (ml_dtypes.float8_e4m3fn, 7), "e5m2": (ml_dtypes.float8_e5m2, 14)}[fmt]
    v = np.moveaxis(np.asarray(x, np.float32).astype(ml_dtypes.bfloat16).astype(np.float64), axis, -1)
    blocks = v.reshape(v.shape[:-1] + (-1, 32))
    amax = np.abs(blocks).max(-1, keepdims=True)
    byte = np.maximum(np.where(amax > 0, np.frexp(amax)[1] - 1 + 127, 0) - down, 1)
    scale = np.exp2(byte - 127.0)
    codes = (blocks / scale).astype(np.float32).astype(dtype).astype(np.float64)
    return np.moveaxis((codes * scale).reshape(v.shape), -1, axis)


WIDE = False


def mx_kscale(k):
    if not WIDE:
        return np.ones(k)
    levels = np.array([10, -10, 5, -5, 0])
    if k % 512:
        return np.exp2(np.random.permutation(np.resize(levels, k // 32))).repeat(32)
    a = np.empty((k // 512, 16))
    for p in range(k // 512):
        a[p, :8] = np.random.permutation(np.resize(levels, 8))
        for g in range(8):
            far = levels[np.abs(levels - a[p, g]) >= 10]
            a[p, g + 8] = far[np.random.randint(len(far))]
    return np.exp2(a.ravel()).repeat(32)


BF16 = ml_dtypes.bfloat16


def bf(x):
    return np.asarray(x, np.float32).astype(BF16)


def f64(x):
    return np.asarray(x).astype(np.float64)


B, S, HID, NH, NOPE, ROPE, VD, KV_RANK, SW, QB = 1, 2048, 1024, 8, 64, 128, 128, 512, 384, 128
QK = NOPE + ROPE


def rotate_half(x):
    h = x.shape[-1] // 2
    return np.concatenate([-x[..., h:], x[..., :h]], axis=-1)


def rope_tables():
    pos = np.arange(S, dtype=np.float64)
    inv = 1.0 / (10000.0 ** (np.arange(0, ROPE, 2, dtype=np.float64) / ROPE))
    ang = pos[:, None] * inv[None, :]
    ang = np.concatenate([ang, ang], axis=-1)
    return bf(np.broadcast_to(np.cos(ang)[None], (B, S, ROPE))), bf(np.broadcast_to(np.sin(ang)[None], (B, S, ROPE)))


def setup_inputs():
    s = mx_kscale(HID)
    cos, sin = rope_tables()
    return {"hidden_states": bf(np.random.standard_normal((B, S, HID)) * s), "cos": cos, "sin": sin,
            "Wq": bf(np.random.standard_normal((HID, NH * QK)) * 2.0 / np.sqrt(HID) / s[:, None]),
            "bq": bf(np.random.standard_normal(NH * QK) * 0.2)}


def core(hidden_states, cos, sin, Wq, bq):
    q = ((mxq(f64(hidden_states), 2, "e4m3") @ mxq(f64(Wq), 0, "e4m3")) + f64(bq)).reshape(B, S, NH, QK).transpose(0, 2, 1, 3)
    q_nope, q_rope = q[..., :NOPE], q[..., NOPE:]
    c, si = f64(cos)[:, None], f64(sin)[:, None]
    q_rope = q_rope * c + rotate_half(q_rope) * si
    return np.concatenate([q_nope, q_rope], axis=-1)


def e4m3fn_bytes(y):
    return np.clip(np.asarray(y, np.float64), -448.0, 448.0).astype(np.float32).astype(ml_dtypes.float8_e4m3fn).view(np.uint8)


def reference(hidden_states, cos, sin, Wq, bq):
    out = core(hidden_states, cos, sin, Wq, bq)
    s = np.max(np.abs(out), axis=-1, keepdims=True) / 448.0
    return out, e4m3fn_bytes(out / s)

@@ -1,0 +1,304 @@
+from contextlib import ExitStack
+
+import concourse.mybir as mybir
+from concourse.masks import make_identity
+
+F32 = mybir.dt.float32
+BF16 = mybir.dt.bfloat16
+U32 = mybir.dt.uint32
+U8 = mybir.dt.uint8
+FP8X4 = mybir.dt.float8_e4m3fn_x4
+FP8 = mybir.dt.float8_e4m3fn
+ACT = mybir.ActivationFunctionType
+ALU = mybir.AluOpType
+AX = mybir.AxisListType
+
+S, HID, NH, NOPE, ROPE = 2048, 1024, 8, 64, 128
+QK = NOPE + ROPE
+FLOPS = 2 * S * HID * NH * QK
+
+P = 128
+NQ = 4
+NI = 4
+NG = NQ * NI
+
+
+def tile_gptossmlaattention_pb_kernel(tc, hidden_states, cos, sin, Wq, bq, out_0, out_1):
+    nc = tc.nc
+    with ExitStack() as ctx:
+        keep = ctx.enter_context(tc.tile_pool(name="keep", bufs=1))
+        stage = ctx.enter_context(tc.tile_pool(name="stage", bufs=2))
+        xpool = ctx.enter_context(tc.tile_pool(name="xpool", bufs=6))
+        tmp = ctx.enter_context(tc.tile_pool(name="tmp", bufs=3))
+        opool = ctx.enter_context(tc.tile_pool(name="opool", bufs=4))
+        pm = ctx.enter_context(tc.psum_pool(name="pm", bufs=3))
+        pt = ctx.enter_context(tc.psum_pool(name="pt", bufs=3))
+        ph = ctx.enter_context(tc.psum_pool(name="ph", bufs=2))
+
+        hid = [keep.tile([P, 4, HID], BF16, name="hid%d" % q) for q in range(NQ)]
+        wraw = [keep.tile([P, 2, 4, 384], BF16, name="wraw%d" % i) for i in range(NI)]
+        cosr = keep.tile([P, NQ, 4, ROPE], BF16, name="cosr")
+        sinr = keep.tile([P, NQ, 4, ROPE], BF16, name="sinr")
+        brow = keep.tile([P, P], BF16, name="brow")
+
+        def load_hid(q, k0, k1):
+            nc.sync.dma_start(
+                out=hid[q][:, :, k0:k1],
+                in_=hidden_states[0, 512 * q : 512 * (q + 1), k0:k1].rearrange("(p j) k -> p j k", j=4),
+            )
+
+        def load_w(i, g):
+            nc.sync.dma_start(
+                out=wraw[i][:, g, :, :],
+                in_=Wq[512 * g : 512 * (g + 1), 384 * i : 384 * (i + 1)].rearrange("(p t) c -> p t c", t=4),
+            )
+
+        def load_tab(dst, src, q0, q1):
+            nc.sync.dma_start(
+                out=dst[:, q0:q1, :, :].rearrange("p q j d -> p q (j d)"),
+                in_=src[0, 512 * q0 : 512 * q1, :].rearrange("(q p j) d -> p q (j d)", p=P, j=4),
+            )
+
+        nc.vector.memset(brow[:], 0.0)
+        load_hid(0, 0, 512)
+        load_w(0, 0)
+        load_hid(0, 512, 1024)
+        load_w(0, 1)
+        nc.sync.dma_start(out=brow[0:8, :], in_=bq.rearrange("(h e) -> h e", e=QK)[:, NOPE:QK])
+        nc.sync.dma_start(
+            out=brow[8:12, :].rearrange("i (hh e) -> i hh e", e=NOPE),
+            in_=bq.rearrange("(i hh e) -> i hh e", hh=2, e=QK)[:, :, 0:NOPE],
+        )
+        load_tab(sinr, sin, 0, 1)
+        load_tab(cosr, cos, 0, 1)
+        load_w(1, 0)
+        load_w(1, 1)
+        load_hid(1, 0, HID)
+        load_w(2, 0)
+        load_w(2, 1)
+        load_w(3, 0)
+        load_w(3, 1)
+        load_tab(sinr, sin, 1, NQ)
+        load_tab(cosr, cos, 1, NQ)
+        load_hid(2, 0, HID)
+        load_hid(3, 0, HID)
+
+        ident = keep.tile([P, P], F32, name="ident")
+        make_identity(nc, ident[:])
+        zero = keep.tile([P, 1], F32, name="zero")
+        nc.vector.memset(zero[:], 0.0)
+
+        browf = keep.tile([P, P], F32, name="browf")
+        nc.vector.tensor_copy(out=browf[:], in_=brow[:])
+        bt = ph.tile([P, 512], F32, tag="h")
+        nc.tensor.transpose(bt[:, 0:P], browf[:], ident[:])
+        bias = keep.tile([P, 12], F32, name="bias")
+        nc.vector.tensor_copy(out=bias[:], in_=bt[:, 0:12])
+
+        sinw = keep.tile([P, NQ, 4, ROPE], BF16, name="sinw")
+
+        def build_sinw(q0, q1):
+            for lo, hi, sign in ((0, 64, 1.0), (64, 0, -1.0)):
+                nc.gpsimd.tensor_scalar(
+                    out=sinw[:, q0:q1, :, lo : lo + 64].rearrange("p q j d -> p (q j) d"),
+                    in0=sinr[:, q0:q1, :, hi : hi + 64].rearrange("p q j d -> p (q j) d"),
+                    scalar1=sign, scalar2=0.0, op0=ALU.mult, op1=ALU.add,
+                )
+
+        wr = [keep.tile([P, 512], U32, name="wr%d" % i, align_bytes=64) for i in range(NI)]
+        wrs = [keep.tile([P, 512], U8, name="wrs%d" % i, align_bytes=64) for i in range(NI)]
+        wn = [keep.tile([P, 256], U32, name="wn%d" % i, align_bytes=64) for i in range(NI)]
+        wns = [keep.tile([P, 256], U8, name="wns%d" % i, align_bytes=64) for i in range(NI)]
+
+        def interleave(eng_name, out, in_):
+            if eng_name == "v":
+                nc.vector.tensor_copy(out=out, in_=in_)
+            elif eng_name == "s":
+                nc.scalar.copy(out=out, in_=in_)
+            else:
+                nc.gpsimd.tensor_scalar(out=out, in0=in_, scalar1=1.0, scalar2=0.0, op0=ALU.mult, op1=ALU.add)
+
+        wstate = {}
+
+        def prep_w_copy(i, g, eng_name):
+            if g == 0:
+                grp_r = stage.tile([P, 2, 256, 4], BF16, tag="grp_r", align_bytes=64)
+                grp_n = stage.tile([P, 2, 128, 4], BF16, tag="grp_n", align_bytes=64)
+                wstate[i] = (grp_r, grp_n)
+            grp_r, grp_n = wstate[i]
+            src = wraw[i][:, g, :, :].rearrange("p t (hh e) -> p hh e t", hh=2)
+            interleave(eng_name, grp_r[:, g, :, :].rearrange("p (hh d) t -> p hh d t", hh=2), src[:, :, NOPE:QK, :])
+            interleave(eng_name, grp_n[:, g, :, :].rearrange("p (hh e) t -> p hh e t", hh=2), src[:, :, 0:NOPE, :])
+
+        def prep_w_quant(i, g0, g1):
+            grp_r, grp_n = wstate[i]
+            nc.vector.quantize_mx(
+                out=wr[i][:, 256 * g0 : 256 * g1].bitcast(FP8X4), scales=wrs[i][:, 256 * g0 : 256 * g1],
+                in_=grp_r[:, g0:g1, :, :].rearrange("p g c t -> p (g c t)"),
+            )
+            nc.vector.quantize_mx(
+                out=wn[i][:, 128 * g0 : 128 * g1].bitcast(FP8X4), scales=wns[i][:, 128 * g0 : 128 * g1],
+                in_=grp_n[:, g0:g1, :, :].rearrange("p g c t -> p (g c t)"),
+            )
+
+        hstate = {}
+
+        def prep_h_alloc(q):
+            grp_h = stage.tile([P, 2, 2048], BF16, tag="grp_h", align_bytes=64)
+            hc = stage.tile([P, 2, 512], U32, tag="hc", align_bytes=64)
+            hs = stage.tile([P, 2, 512], U8, tag="hs", align_bytes=64)
+            hstate[q] = (grp_h, hc, hs)
+
+        def prep_h_part(q, g, jp):
+            grp_h, hc, hs = hstate[q]
+            words = hid[q][:].bitcast(F32)
+            ht = ph.tile([P, 2, 2, P], F32, tag="h")
+            for jj in range(2):
+                for u in range(2):
+                    nc.tensor.transpose(
+                        ht[:, jj, u, :], words[:, 2 * jp + jj, 256 * g + u : 256 * (g + 1) : 2], ident[:]
+                    )
+            nc.scalar.copy(
+                out=grp_h[:].bitcast(F32)[:, g, 512 * jp : 512 * (jp + 1)].rearrange(
+                    "p (jj c u) -> p jj c u", jj=2, u=2
+                ),
+                in_=ht[:].rearrange("p jj u c -> p jj c u"),
+            )
+            if jp == 1:
+                nc.vector.quantize_mx(out=hc[:, g, :].bitcast(FP8X4), scales=hs[:, g, :], in_=grp_h[:, g, :])
+
+        gstate = {}
+
+        def mx_evac(n):
+            q, i = divmod(n, NI)
+            grp_h, hc, hs = hstate[q]
+            xts = []
+            ms = []
+            for u in range(3):
+                m = pm.tile([P, 512], F32, tag="m")
+                ms.append(m)
+
+            def one_pass(u, g):
+                if u > 0:
+                    cod, sca, w0, wstep = wr[i], wrs[i], 128 * (u - 1), 256
+                else:
+                    cod, sca, w0, wstep = wn[i], wns[i], 0, 128
+                cols = slice(w0 + wstep * g, w0 + wstep * g + 128)
+                nc.tensor.matmul_mx(
+                    out=ms[u][:],
+                    lhsT=cod[:, cols].bitcast(FP8X4),
+                    lhsT_scale=sca[:, cols],
+                    rhs=hc[:, g, :].bitcast(FP8X4),
+                    rhs_scale=hs[:, g, :],
+                    start=(g == 0),
+                    stop=(g == 1),
+                )
+
+            if n == 0:
+                for g in range(2):
+                    for u in range(3):
+                        one_pass(u, g)
+            else:
+                for u in range(3):
+                    for g in range(2):
+                        one_pass(u, g)
+            for u in range(3):
+                bcol = 8 + i if u == 0 else 2 * i + u - 1
+                xt = xpool.tile([P, 512], F32, tag="xt")
+                nc.scalar.activation(
+                    out=xt[:], in_=ms[u][:], func=ACT.Identity, bias=bias[:, bcol : bcol + 1], scale=1.0
+                )
+                xts.append(xt)
+            gstate[n] = xts
+
+        def back_rope(n):
+            q, i = divmod(n, NI)
+            xts = gstate[n]
+            o = opool.tile([P, 2, 4, QK], F32, tag="o")
+            ts = []
+            for u in range(3):
+                t = pt.tile([P, 4, P], F32, tag="t")
+                for j in range(4):
+                    nc.tensor.transpose(t[:, j, :], xts[u][:, 128 * j : 128 * (j + 1)], ident[:])
+                ts.append(t)
+            nc.scalar.copy(out=o[:, :, :, 0:NOPE], in_=ts[0][:].rearrange("p j (hh e) -> p hh j e", hh=2))
+            for hh in range(2):
+                t = ts[hh + 1]
+                ta = tmp.tile([P, 4, ROPE], F32, tag="ta")
+                tb = tmp.tile([P, 4, ROPE], F32, tag="tb")
+                nc.vector.tensor_tensor(out=ta[:], in0=t[:], in1=cosr[:, q, :, :], op=ALU.mult)
+                nc.vector.tensor_tensor(out=tb[:], in0=t[:], in1=sinw[:, q, :, :], op=ALU.mult)
+                nc.gpsimd.tensor_tensor(
+                    out=o[:, hh, :, NOPE : NOPE + 64], in0=ta[:, :, 0:64], in1=tb[:, :, 64:128], op=ALU.add
+                )
+                nc.gpsimd.tensor_tensor(
+                    out=o[:, hh, :, NOPE + 64 : QK], in0=ta[:, :, 64:128], in1=tb[:, :, 0:64], op=ALU.add
+                )
+            gstate[n] = o
+
+        def fin(n):
+            q, i = divmod(n, NI)
+            o = gstate[n]
+            am = tmp.tile([P, 8], F32, tag="am")
+            rc = tmp.tile([P, 8], F32, tag="rc")
+            r4 = tmp.tile([P, 8], F32, tag="r4")
+            last = n >= NG - 1
+            pieces = ((0, 4), (4, 8)) if last else ((0, 8),)
+            for k0, k1 in pieces:
+                nc.vector.tensor_reduce(
+                    out=am[:, k0:k1], in_=o[:].rearrange("p hh j e -> p (hh j) e")[:, k0:k1, :], axis=AX.X, op=ALU.max,
+                    apply_absolute_value=True,
+                )
+                nc.vector.reciprocal(out=rc[:, k0:k1], in_=am[:, k0:k1])
+                nc.gpsimd.tensor_scalar(
+                    out=r4[:, k0:k1], in0=rc[:, k0:k1], scalar1=448.0, scalar2=0.0, op0=ALU.mult, op1=ALU.add
+                )
+            nc.sync.dma_start(
+                out=out_0[0, 2 * i : 2 * i + 2, 512 * q : 512 * (q + 1), :].rearrange("h (p j) e -> p h (j e)", j=4),
+                in_=o[:].rearrange("p hh j e -> p hh (j e)"),
+            )
+            f8 = opool.tile([P, 2, 4, QK], FP8, tag="f8")
+            for hh in range(2):
+                for j in range(4):
+                    k = 4 * hh + j
+                    if n >= NG - 2 and j >= 2:
+                        nc.vector.tensor_scalar(
+                            out=f8[:, hh, j, :], in0=o[:, hh, j, :], scalar1=r4[:, k : k + 1], scalar2=None,
+                            op0=ALU.mult, saturate=False,
+                        )
+                    else:
+                        nc.scalar.activation(
+                            out=f8[:, hh, j, :], in_=o[:, hh, j, :], func=ACT.Identity,
+                            scale=r4[:, k : k + 1], bias=zero[:, 0:1], saturate=False,
+                        )
+                nc.sync.dma_start(
+                    out=out_1[0, 2 * i + hh, 512 * q : 512 * (q + 1), :].rearrange("(p j) e -> p (j e)", j=4),
+                    in_=f8[:, hh, :, :].rearrange("p j e -> p (j e)").bitcast(U8),
+                )
+
+        prep_h_alloc(0)
+        for g in range(2):
+            prep_w_copy(0, g, "v")
+            prep_h_part(0, g, 0)
+            prep_w_quant(0, g, g + 1)
+            prep_h_part(0, g, 1)
+        build_sinw(0, 1)
+        for n in range(NG + 2):
+            q, i = divmod(n, NI)
+            if n < NG:
+                mx_evac(n)
+                if q == 0 and i + 1 < NI:
+                    prep_w_copy(i + 1, 0, "g")
+                    prep_w_copy(i + 1, 1, "g")
+                    prep_w_quant(i + 1, 0, 2)
+                if n == 1:
+                    build_sinw(1, NQ)
+                if q + 1 < NQ and i < 2:
+                    if i == 0:
+                        prep_h_alloc(q + 1)
+                    prep_h_part(q + 1, i, 0)
+                    prep_h_part(q + 1, i, 1)
+            if 0 <= n - 1 < NG:
+                back_rope(n - 1)
+            if 0 <= n - 2 < NG:
+                fin(n - 2)

@@ -28,18 +28,20 @@ def tile_gptossmlaattention_pb_kernel(tc, hidden_states, cos, sin, Wq, bq, out_0
     with ExitStack() as ctx:
         keep = ctx.enter_context(tc.tile_pool(name="keep", bufs=1))
         stage = ctx.enter_context(tc.tile_pool(name="stage", bufs=2))
-        xpool = ctx.enter_context(tc.tile_pool(name="xpool", bufs=6))
+        xpool = ctx.enter_context(tc.tile_pool(name="xpool", bufs=4))
         tmp = ctx.enter_context(tc.tile_pool(name="tmp", bufs=3))
-        opool = ctx.enter_context(tc.tile_pool(name="opool", bufs=4))
-        pm = ctx.enter_context(tc.psum_pool(name="pm", bufs=3))
+        opool = ctx.enter_context(tc.tile_pool(name="opool", bufs=5))
+        pm = ctx.enter_context(tc.psum_pool(name="pm", bufs=2))
+        pn = ctx.enter_context(tc.psum_pool(name="pn", bufs=1))
         pt = ctx.enter_context(tc.psum_pool(name="pt", bufs=3))
         ph = ctx.enter_context(tc.psum_pool(name="ph", bufs=2))
 
         hid = [keep.tile([P, 4, HID], BF16, name="hid%d" % q) for q in range(NQ)]
         wraw = [keep.tile([P, 2, 4, 384], BF16, name="wraw%d" % i) for i in range(NI)]
-        cosr = keep.tile([P, NQ, 4, ROPE], BF16, name="cosr")
+        cs = keep.tile([P, NQ, 2, 4, ROPE], BF16, name="cs")
         sinr = keep.tile([P, NQ, 4, ROPE], BF16, name="sinr")
         brow = keep.tile([P, P], BF16, name="brow")
+        bnrow = keep.tile([P, 512], BF16, name="bnrow")
 
         def load_hid(q, k0, k1):
             nc.sync.dma_start(
@@ -53,24 +55,31 @@ def tile_gptossmlaattention_pb_kernel(tc, hidden_states, cos, sin, Wq, bq, out_0
                 in_=Wq[512 * g : 512 * (g + 1), 384 * i : 384 * (i + 1)].rearrange("(p t) c -> p t c", t=4),
             )
 
-        def load_tab(dst, src, q0, q1):
+        def load_sin(q0, q1):
             nc.sync.dma_start(
-                out=dst[:, q0:q1, :, :].rearrange("p q j d -> p q (j d)"),
-                in_=src[0, 512 * q0 : 512 * q1, :].rearrange("(q p j) d -> p q (j d)", p=P, j=4),
+                out=sinr[:, q0:q1, :, :].rearrange("p q j d -> p q (j d)"),
+                in_=sin[0, 512 * q0 : 512 * q1, :].rearrange("(q p j) d -> p q (j d)", p=P, j=4),
+            )
+
+        def load_cos(q0, q1):
+            nc.sync.dma_start(
+                out=cs[:, q0:q1, 0, :, :].rearrange("p q j d -> p q (j d)"),
+                in_=cos[0, 512 * q0 : 512 * q1, :].rearrange("(q p j) d -> p q (j d)", p=P, j=4),
             )
 
         nc.vector.memset(brow[:], 0.0)
+        nc.gpsimd.memset(bnrow[:], 0.0)
         load_hid(0, 0, 512)
         load_w(0, 0)
         load_hid(0, 512, 1024)
         load_w(0, 1)
         nc.sync.dma_start(out=brow[0:8, :], in_=bq.rearrange("(h e) -> h e", e=QK)[:, NOPE:QK])
         nc.sync.dma_start(
-            out=brow[8:12, :].rearrange("i (hh e) -> i hh e", e=NOPE),
-            in_=bq.rearrange("(i hh e) -> i hh e", hh=2, e=QK)[:, :, 0:NOPE],
+            out=bnrow[0:1, :].rearrange("o (h e) -> o h e", e=NOPE),
+            in_=bq.rearrange("(o h e) -> o h e", o=1, e=QK)[:, :, 0:NOPE],
         )
-        load_tab(sinr, sin, 0, 1)
-        load_tab(cosr, cos, 0, 1)
+        load_sin(0, 1)
+        load_cos(0, 1)
         load_w(1, 0)
         load_w(1, 1)
         load_hid(1, 0, HID)
@@ -78,8 +87,8 @@ def tile_gptossmlaattention_pb_kernel(tc, hidden_states, cos, sin, Wq, bq, out_0
         load_w(2, 1)
         load_w(3, 0)
         load_w(3, 1)
-        load_tab(sinr, sin, 1, NQ)
-        load_tab(cosr, cos, 1, NQ)
+        load_sin(1, NQ)
+        load_cos(1, NQ)
         load_hid(2, 0, HID)
         load_hid(3, 0, HID)
 
@@ -87,21 +96,25 @@ def tile_gptossmlaattention_pb_kernel(tc, hidden_states, cos, sin, Wq, bq, out_0
         make_identity(nc, ident[:])
         zero = keep.tile([P, 1], F32, name="zero")
         nc.vector.memset(zero[:], 0.0)
+        ones = keep.tile([P, P], BF16, name="ones")
+        nc.gpsimd.memset(ones[:], 1.0)
 
         browf = keep.tile([P, P], F32, name="browf")
         nc.vector.tensor_copy(out=browf[:], in_=brow[:])
         bt = ph.tile([P, 512], F32, tag="h")
         nc.tensor.transpose(bt[:, 0:P], browf[:], ident[:])
-        bias = keep.tile([P, 12], F32, name="bias")
-        nc.vector.tensor_copy(out=bias[:], in_=bt[:, 0:12])
-
-        sinw = keep.tile([P, NQ, 4, ROPE], BF16, name="sinw")
+        bias = keep.tile([P, 8], F32, name="bias")
+        nc.vector.tensor_copy(out=bias[:], in_=bt[:, 0:8])
+        bn_ps = ph.tile([P, 512], F32, tag="h")
+        nc.tensor.matmul(out=bn_ps[:], lhsT=ones[:], rhs=bnrow[:], start=True, stop=True)
+        biasn = keep.tile([P, NH, NOPE], F32, name="biasn")
+        nc.vector.tensor_copy(out=biasn[:].rearrange("p h e -> p (h e)"), in_=bn_ps[:])
 
         def build_sinw(q0, q1):
             for lo, hi, sign in ((0, 64, 1.0), (64, 0, -1.0)):
                 nc.gpsimd.tensor_scalar(
-                    out=sinw[:, q0:q1, :, lo : lo + 64].rearrange("p q j d -> p (q j) d"),
-                    in0=sinr[:, q0:q1, :, hi : hi + 64].rearrange("p q j d -> p (q j) d"),
+                    out=cs[:, q0:q1, 1, :, lo : lo + 64],
+                    in0=sinr[:, q0:q1, :, hi : hi + 64],
                     scalar1=sign, scalar2=0.0, op0=ALU.mult, op1=ALU.add,
                 )
 
@@ -128,7 +141,9 @@ def tile_gptossmlaattention_pb_kernel(tc, hidden_states, cos, sin, Wq, bq, out_0
             grp_r, grp_n = wstate[i]
             src = wraw[i][:, g, :, :].rearrange("p t (hh e) -> p hh e t", hh=2)
             interleave(eng_name, grp_r[:, g, :, :].rearrange("p (hh d) t -> p hh d t", hh=2), src[:, :, NOPE:QK, :])
-            interleave(eng_name, grp_n[:, g, :, :].rearrange("p (hh e) t -> p hh e t", hh=2), src[:, :, 0:NOPE, :])
+            interleave(
+                "g" if i == 0 else eng_name, grp_n[:, g, :, :].rearrange("p (hh e) t -> p hh e t", hh=2), src[:, :, 0:NOPE, :]
+            )
 
         def prep_w_quant(i, g0, g1):
             grp_r, grp_n = wstate[i]
@@ -172,22 +187,17 @@ def tile_gptossmlaattention_pb_kernel(tc, hidden_states, cos, sin, Wq, bq, out_0
         def mx_evac(n):
             q, i = divmod(n, NI)
             grp_h, hc, hs = hstate[q]
-            xts = []
             ms = []
-            for u in range(3):
+            for u in range(2):
                 m = pm.tile([P, 512], F32, tag="m")
                 ms.append(m)
 
-            def one_pass(u, g):
-                if u > 0:
-                    cod, sca, w0, wstep = wr[i], wrs[i], 128 * (u - 1), 256
-                else:
-                    cod, sca, w0, wstep = wn[i], wns[i], 0, 128
-                cols = slice(w0 + wstep * g, w0 + wstep * g + 128)
+            def rope_pass(u, g):
+                cols = slice(128 * u + 256 * g, 128 * u + 256 * g + 128)
                 nc.tensor.matmul_mx(
                     out=ms[u][:],
-                    lhsT=cod[:, cols].bitcast(FP8X4),
-                    lhsT_scale=sca[:, cols],
+                    lhsT=wr[i][:, cols].bitcast(FP8X4),
+                    lhsT_scale=wrs[i][:, cols],
                     rhs=hc[:, g, :].bitcast(FP8X4),
                     rhs_scale=hs[:, g, :],
                     start=(g == 0),
@@ -196,43 +206,65 @@ def tile_gptossmlaattention_pb_kernel(tc, hidden_states, cos, sin, Wq, bq, out_0
 
             if n == 0:
                 for g in range(2):
-                    for u in range(3):
-                        one_pass(u, g)
+                    for u in range(2):
+                        rope_pass(u, g)
             else:
-                for u in range(3):
+                for u in range(2):
                     for g in range(2):
-                        one_pass(u, g)
-            for u in range(3):
-                bcol = 8 + i if u == 0 else 2 * i + u - 1
+                        rope_pass(u, g)
+            mn = pn.tile([P, 4, P], F32, tag="mn")
+            for j in range(4):
+                for g in range(2):
+                    tok = slice(128 * j, 128 * (j + 1))
+                    cols = slice(128 * g, 128 * (g + 1))
+                    nc.tensor.matmul_mx(
+                        out=mn[:, j, :],
+                        lhsT=hc[:, g, tok].bitcast(FP8X4),
+                        lhsT_scale=hs[:, g, tok],
+                        rhs=wn[i][:, cols].bitcast(FP8X4),
+                        rhs_scale=wns[i][:, cols],
+                        start=(g == 0),
+                        stop=(g == 1),
+                    )
+            xts = []
+            for u in range(2):
                 xt = xpool.tile([P, 512], F32, tag="xt")
                 nc.scalar.activation(
-                    out=xt[:], in_=ms[u][:], func=ACT.Identity, bias=bias[:, bcol : bcol + 1], scale=1.0
+                    out=xt[:], in_=ms[u][:], func=ACT.Identity, bias=bias[:, 2 * i + u : 2 * i + u + 1], scale=1.0
                 )
                 xts.append(xt)
-            gstate[n] = xts
+            o = opool.tile([P, 2, 4, QK], F32, tag="o")
+            nc.scalar.copy(out=o[:, :, :, 0:NOPE], in_=mn[:].rearrange("p j (hh e) -> p hh j e", hh=2))
+            nc.gpsimd.tensor_tensor(
+                out=o[:, :, :, 0:NOPE], in0=o[:, :, :, 0:NOPE],
+                in1=biasn[:, 2 * i : 2 * i + 2, :].unsqueeze(2).to_broadcast([P, 2, 4, NOPE]), op=ALU.add,
+            )
+            gstate[n] = (xts, o)
 
         def back_rope(n):
             q, i = divmod(n, NI)
-            xts = gstate[n]
-            o = opool.tile([P, 2, 4, QK], F32, tag="o")
-            ts = []
-            for u in range(3):
+            xts, o = gstate[n]
+            tab = tmp.tile([P, 2, 2, 4, ROPE], F32, tag="tab")
+            for hh in range(2):
                 t = pt.tile([P, 4, P], F32, tag="t")
                 for j in range(4):
-                    nc.tensor.transpose(t[:, j, :], xts[u][:, 128 * j : 128 * (j + 1)], ident[:])
-                ts.append(t)
-            nc.scalar.copy(out=o[:, :, :, 0:NOPE], in_=ts[0][:].rearrange("p j (hh e) -> p hh j e", hh=2))
-            for hh in range(2):
-                t = ts[hh + 1]
-                ta = tmp.tile([P, 4, ROPE], F32, tag="ta")
-                tb = tmp.tile([P, 4, ROPE], F32, tag="tb")
-                nc.vector.tensor_tensor(out=ta[:], in0=t[:], in1=cosr[:, q, :, :], op=ALU.mult)
-                nc.vector.tensor_tensor(out=tb[:], in0=t[:], in1=sinw[:, q, :, :], op=ALU.mult)
+                    nc.tensor.transpose(t[:, j, :], xts[hh][:, 128 * j : 128 * (j + 1)], ident[:])
+                nc.vector.tensor_tensor(
+                    out=tab[:, hh, :, :, :].rearrange("p c j d -> p c (j d)"),
+                    in0=t[:].rearrange("p j d -> p (j d)").unsqueeze(1).to_broadcast([P, 2, 512]),
+                    in1=cs[:, q, :, :, :].rearrange("p c j d -> p c (j d)"),
+                    op=ALU.mult,
+                )
+            last = n >= NG - 1
+            heads = ((0, 1), (1, 2)) if last else ((0, 2),)
+            for h0, h1 in heads:
                 nc.gpsimd.tensor_tensor(
-                    out=o[:, hh, :, NOPE : NOPE + 64], in0=ta[:, :, 0:64], in1=tb[:, :, 64:128], op=ALU.add
+                    out=o[:, h0:h1, :, NOPE : NOPE + 64], in0=tab[:, h0:h1, 0, :, 0:64], in1=tab[:, h0:h1, 1, :, 64:128],
+                    op=ALU.add,
                 )
                 nc.gpsimd.tensor_tensor(
-                    out=o[:, hh, :, NOPE + 64 : QK], in0=ta[:, :, 64:128], in1=tb[:, :, 0:64], op=ALU.add
+                    out=o[:, h0:h1, :, NOPE + 64 : QK], in0=tab[:, h0:h1, 0, :, 64:128], in1=tab[:, h0:h1, 1, :, 0:64],
+                    op=ALU.add,
                 )
             gstate[n] = o
 
@@ -250,9 +282,7 @@ def tile_gptossmlaattention_pb_kernel(tc, hidden_states, cos, sin, Wq, bq, out_0
                     apply_absolute_value=True,
                 )
                 nc.vector.reciprocal(out=rc[:, k0:k1], in_=am[:, k0:k1])
-                nc.gpsimd.tensor_scalar(
-                    out=r4[:, k0:k1], in0=rc[:, k0:k1], scalar1=448.0, scalar2=0.0, op0=ALU.mult, op1=ALU.add
-                )
+                nc.scalar.activation(out=r4[:, k0:k1], in_=rc[:, k0:k1], func=ACT.Copy, scale=448.0)
             nc.sync.dma_start(
                 out=out_0[0, 2 * i : 2 * i + 2, 512 * q : 512 * (q + 1), :].rearrange("h (p j) e -> p h (j e)", j=4),
                 in_=o[:].rearrange("p hh j e -> p hh (j e)"),
@@ -283,14 +313,17 @@ def tile_gptossmlaattention_pb_kernel(tc, hidden_states, cos, sin, Wq, bq, out_0
             prep_w_quant(0, g, g + 1)
             prep_h_part(0, g, 1)
         build_sinw(0, 1)
+        prep_w_copy(1, 0, "v")
+        prep_w_copy(1, 1, "v")
+        prep_w_quant(1, 0, 2)
         for n in range(NG + 2):
             q, i = divmod(n, NI)
             if n < NG:
                 mx_evac(n)
-                if q == 0 and i + 1 < NI:
-                    prep_w_copy(i + 1, 0, "g")
-                    prep_w_copy(i + 1, 1, "g")
-                    prep_w_quant(i + 1, 0, 2)
+                if q == 0 and 1 <= i + 1 < NI - 1:
+                    prep_w_copy(i + 2, 0, "sg"[i])
+                    prep_w_copy(i + 2, 1, "sg"[i])
+                    prep_w_quant(i + 2, 0, 2)
                 if n == 1:
                     build_sinw(1, NQ)
                 if q + 1 < NQ and i < 2:

@@ -142,7 +142,7 @@ def tile_gptossmlaattention_pb_kernel(tc, hidden_states, cos, sin, Wq, bq, out_0
             src = wraw[i][:, g, :, :].rearrange("p t (hh e) -> p hh e t", hh=2)
             interleave(eng_name, grp_r[:, g, :, :].rearrange("p (hh d) t -> p hh d t", hh=2), src[:, :, NOPE:QK, :])
             interleave(
-                "g" if i == 0 else eng_name, grp_n[:, g, :, :].rearrange("p (hh e) t -> p hh e t", hh=2), src[:, :, 0:NOPE, :]
+                "s" if i == 0 else eng_name, grp_n[:, g, :, :].rearrange("p (hh e) t -> p hh e t", hh=2), src[:, :, 0:NOPE, :]
             )
 
         def prep_w_quant(i, g0, g1):
@@ -313,8 +313,8 @@ def tile_gptossmlaattention_pb_kernel(tc, hidden_states, cos, sin, Wq, bq, out_0
             prep_w_quant(0, g, g + 1)
             prep_h_part(0, g, 1)
         build_sinw(0, 1)
-        prep_w_copy(1, 0, "v")
-        prep_w_copy(1, 1, "v")
+        prep_w_copy(1, 0, "s")
+        prep_w_copy(1, 1, "s")
         prep_w_quant(1, 0, 2)
         for n in range(NG + 2):
             q, i = divmod(n, NI)

@@ -31,9 +31,9 @@ def tile_gptossmlaattention_pb_kernel(tc, hidden_states, cos, sin, Wq, bq, out_0
         xpool = ctx.enter_context(tc.tile_pool(name="xpool", bufs=4))
         tmp = ctx.enter_context(tc.tile_pool(name="tmp", bufs=3))
         opool = ctx.enter_context(tc.tile_pool(name="opool", bufs=5))
-        pm = ctx.enter_context(tc.psum_pool(name="pm", bufs=2))
+        pm = ctx.enter_context(tc.psum_pool(name="pm", bufs=3))
         pn = ctx.enter_context(tc.psum_pool(name="pn", bufs=1))
-        pt = ctx.enter_context(tc.psum_pool(name="pt", bufs=3))
+        pt = ctx.enter_context(tc.psum_pool(name="pt", bufs=2))
         ph = ctx.enter_context(tc.psum_pool(name="ph", bufs=2))
 
         hid = [keep.tile([P, 4, HID], BF16, name="hid%d" % q) for q in range(NQ)]

@@ -266,6 +266,12 @@ def tile_gptossmlaattention_pb_kernel(tc, hidden_states, cos, sin, Wq, bq, out_0
                     out=o[:, h0:h1, :, NOPE + 64 : QK], in0=tab[:, h0:h1, 0, :, 64:128], in1=tab[:, h0:h1, 1, :, 0:64],
                     op=ALU.add,
                 )
+                nc.sync.dma_start(
+                    out=out_0[0, 2 * i + h0 : 2 * i + h1, 512 * q : 512 * (q + 1), :].rearrange(
+                        "h (p j) e -> p h (j e)", j=4
+                    ),
+                    in_=o[:, h0:h1, :, :].rearrange("p hh j e -> p hh (j e)"),
+                )
             gstate[n] = o
 
         def fin(n):
@@ -283,10 +289,6 @@ def tile_gptossmlaattention_pb_kernel(tc, hidden_states, cos, sin, Wq, bq, out_0
                 )
                 nc.vector.reciprocal(out=rc[:, k0:k1], in_=am[:, k0:k1])
                 nc.scalar.activation(out=r4[:, k0:k1], in_=rc[:, k0:k1], func=ACT.Copy, scale=448.0)
-            nc.sync.dma_start(
-                out=out_0[0, 2 * i : 2 * i + 2, 512 * q : 512 * (q + 1), :].rearrange("h (p j) e -> p h (j e)", j=4),
-                in_=o[:].rearrange("p hh j e -> p hh (j e)"),
-            )
             f8 = opool.tile([P, 2, 4, QK], FP8, tag="f8")
             for hh in range(2):
                 for j in range(4):

@@ -21,6 +21,8 @@ P = 128
 NQ = 4
 NI = 4
 NG = NQ * NI
+CAST_LAG = 3
+N_WARM = 5
 
 
 def tile_gptossmlaattention_pb_kernel(tc, hidden_states, cos, sin, Wq, bq, out_0, out_1):
@@ -28,13 +30,16 @@ def tile_gptossmlaattention_pb_kernel(tc, hidden_states, cos, sin, Wq, bq, out_0
     with ExitStack() as ctx:
         keep = ctx.enter_context(tc.tile_pool(name="keep", bufs=1))
         stage = ctx.enter_context(tc.tile_pool(name="stage", bufs=2))
+        wstage = ctx.enter_context(tc.tile_pool(name="wstage", bufs=4))
         xpool = ctx.enter_context(tc.tile_pool(name="xpool", bufs=4))
         tmp = ctx.enter_context(tc.tile_pool(name="tmp", bufs=3))
-        opool = ctx.enter_context(tc.tile_pool(name="opool", bufs=5))
+        stat = ctx.enter_context(tc.tile_pool(name="stat", bufs=5))
+        opool = ctx.enter_context(tc.tile_pool(name="opool", bufs=6))
         pm = ctx.enter_context(tc.psum_pool(name="pm", bufs=3))
         pn = ctx.enter_context(tc.psum_pool(name="pn", bufs=1))
         pt = ctx.enter_context(tc.psum_pool(name="pt", bufs=2))
         ph = ctx.enter_context(tc.psum_pool(name="ph", bufs=2))
+        ctx.enter_context(tc.manual_schedule())
 
         hid = [keep.tile([P, 4, HID], BF16, name="hid%d" % q) for q in range(NQ)]
         wraw = [keep.tile([P, 2, 4, 384], BF16, name="wraw%d" % i) for i in range(NI)]
@@ -42,6 +47,17 @@ def tile_gptossmlaattention_pb_kernel(tc, hidden_states, cos, sin, Wq, bq, out_0
         sinr = keep.tile([P, NQ, 4, ROPE], BF16, name="sinr")
         brow = keep.tile([P, P], BF16, name="brow")
         bnrow = keep.tile([P, 512], BF16, name="bnrow")
+        warm = keep.tile([P, 512], BF16, name="warm")
+        ident = keep.tile([P, P], F32, name="ident")
+        zero = keep.tile([P, 1], F32, name="zero")
+        ones = keep.tile([P, P], BF16, name="ones")
+        identb = keep.tile([P, P], BF16, name="identb")
+        bias = keep.tile([P, 8], F32, name="bias")
+        biasn = keep.tile([P, NH, NOPE], F32, name="biasn")
+        wr = [keep.tile([P, 512], U32, name="wr%d" % i, align_bytes=64) for i in range(NI)]
+        wrs = [keep.tile([P, 512], U8, name="wrs%d" % i, align_bytes=64) for i in range(NI)]
+        wn = [keep.tile([P, 256], U32, name="wn%d" % i, align_bytes=64) for i in range(NI)]
+        wns = [keep.tile([P, 256], U8, name="wns%d" % i, align_bytes=64) for i in range(NI)]
 
         def load_hid(q, k0, k1):
             nc.sync.dma_start(
@@ -67,61 +83,48 @@ def tile_gptossmlaattention_pb_kernel(tc, hidden_states, cos, sin, Wq, bq, out_0
                 in_=cos[0, 512 * q0 : 512 * q1, :].rearrange("(q p j) d -> p q (j d)", p=P, j=4),
             )
 
+        nc.vector.memset(warm[:], 0.0)
         nc.vector.memset(brow[:], 0.0)
         nc.gpsimd.memset(bnrow[:], 0.0)
+        nc.scalar.dma_start(out=brow[0:8, :], in_=bq.rearrange("(h e) -> h e", e=QK)[:, NOPE:QK])
+        nc.scalar.dma_start(
+            out=bnrow[0:1, :].rearrange("o (h e) -> o h e", e=NOPE),
+            in_=bq.rearrange("(o h e) -> o h e", o=1, e=QK)[:, :, 0:NOPE],
+        )
         load_hid(0, 0, 512)
         load_w(0, 0)
         load_hid(0, 512, 1024)
         load_w(0, 1)
-        nc.sync.dma_start(out=brow[0:8, :], in_=bq.rearrange("(h e) -> h e", e=QK)[:, NOPE:QK])
-        nc.sync.dma_start(
-            out=bnrow[0:1, :].rearrange("o (h e) -> o h e", e=NOPE),
-            in_=bq.rearrange("(o h e) -> o h e", o=1, e=QK)[:, :, 0:NOPE],
-        )
-        load_sin(0, 1)
-        load_cos(0, 1)
         load_w(1, 0)
         load_w(1, 1)
-        load_hid(1, 0, HID)
+        load_sin(0, 1)
+        load_cos(0, 1)
         load_w(2, 0)
         load_w(2, 1)
         load_w(3, 0)
         load_w(3, 1)
+        load_hid(1, 0, HID)
         load_sin(1, NQ)
         load_cos(1, NQ)
         load_hid(2, 0, HID)
         load_hid(3, 0, HID)
 
-        ident = keep.tile([P, P], F32, name="ident")
         make_identity(nc, ident[:])
-        zero = keep.tile([P, 1], F32, name="zero")
+        make_identity(nc, identb[:])
         nc.vector.memset(zero[:], 0.0)
-        ones = keep.tile([P, P], BF16, name="ones")
         nc.gpsimd.memset(ones[:], 1.0)
 
-        browf = keep.tile([P, P], F32, name="browf")
-        nc.vector.tensor_copy(out=browf[:], in_=brow[:])
-        bt = ph.tile([P, 512], F32, tag="h")
-        nc.tensor.transpose(bt[:, 0:P], browf[:], ident[:])
-        bias = keep.tile([P, 8], F32, name="bias")
-        nc.vector.tensor_copy(out=bias[:], in_=bt[:, 0:8])
-        bn_ps = ph.tile([P, 512], F32, tag="h")
-        nc.tensor.matmul(out=bn_ps[:], lhsT=ones[:], rhs=bnrow[:], start=True, stop=True)
-        biasn = keep.tile([P, NH, NOPE], F32, name="biasn")
-        nc.vector.tensor_copy(out=biasn[:].rearrange("p h e -> p (h e)"), in_=bn_ps[:])
+        wps = pm.tile([P, 512], F32, tag="m")
+        for rep_i in range(N_WARM):
+            nc.tensor.matmul(out=wps[:], lhsT=warm[:, 0:P], rhs=warm[:], start=True, stop=True)
 
-        def build_sinw(q0, q1):
-            for lo, hi, sign in ((0, 64, 1.0), (64, 0, -1.0)):
-                nc.gpsimd.tensor_scalar(
-                    out=cs[:, q0:q1, 1, :, lo : lo + 64],
-                    in0=sinr[:, q0:q1, :, hi : hi + 64],
-                    scalar1=sign, scalar2=0.0, op0=ALU.mult, op1=ALU.add,
-                )
-
-        wr = [keep.tile([P, 512], U32, name="wr%d" % i, align_bytes=64) for i in range(NI)]
-        wrs = [keep.tile([P, 512], U8, name="wrs%d" % i, align_bytes=64) for i in range(NI)]
-        wn = [keep.tile([P, 256], U32, name="wn%d" % i, align_bytes=64) for i in range(NI)]
-        wns = [keep.tile([P, 256], U8, name="wns%d" % i, align_bytes=64) for i in range(NI)]
+        def build_sinw(q0, q1, half):
+            lo, hi, sign = ((0, 64, 1.0), (64, 0, -1.0))[half]
+            nc.gpsimd.tensor_scalar(
+                out=cs[:, q0:q1, 1, :, lo : lo + 64],
+                in0=sinr[:, q0:q1, :, hi : hi + 64],
+                scalar1=sign, scalar2=0.0, op0=ALU.mult, op1=ALU.add,
+            )
 
         def interleave(eng_name, out, in_):
             if eng_name == "v":
@@ -133,39 +136,39 @@ def tile_gptossmlaattention_pb_kernel(tc, hidden_states, cos, sin, Wq, bq, out_0
 
         wstate = {}
 
-        def prep_w_copy(i, g, eng_name):
-            if g == 0:
-                grp_r = stage.tile([P, 2, 256, 4], BF16, tag="grp_r", align_bytes=64)
-                grp_n = stage.tile([P, 2, 128, 4], BF16, tag="grp_n", align_bytes=64)
-                wstate[i] = (grp_r, grp_n)
-            grp_r, grp_n = wstate[i]
-            src = wraw[i][:, g, :, :].rearrange("p t (hh e) -> p hh e t", hh=2)
-            interleave(eng_name, grp_r[:, g, :, :].rearrange("p (hh d) t -> p hh d t", hh=2), src[:, :, NOPE:QK, :])
-            interleave(
-                "s" if i == 0 else eng_name, grp_n[:, g, :, :].rearrange("p (hh e) t -> p hh e t", hh=2), src[:, :, 0:NOPE, :]
-            )
+        def w_alloc(i):
+            grp_r = wstage.tile([P, 2, 256, 4], BF16, tag="grp_r", align_bytes=64)
+            grp_n = wstage.tile([P, 2, 128, 4], BF16, tag="grp_n", align_bytes=64)
+            wstate[i] = (grp_r, grp_n)
 
-        def prep_w_quant(i, g0, g1):
-            grp_r, grp_n = wstate[i]
+        def w_il_r(i, g, eng_name):
+            src = wraw[i][:, g, :, :].rearrange("p t (hh e) -> p hh e t", hh=2)
+            interleave(eng_name, wstate[i][0][:, g, :, :].rearrange("p (hh d) t -> p hh d t", hh=2), src[:, :, NOPE:QK, :])
+
+        def w_il_n(i, g, eng_name):
+            src = wraw[i][:, g, :, :].rearrange("p t (hh e) -> p hh e t", hh=2)
+            interleave(eng_name, wstate[i][1][:, g, :, :].rearrange("p (hh e) t -> p hh e t", hh=2), src[:, :, 0:NOPE, :])
+
+        def w_q_r(i, g0, g1):
             nc.vector.quantize_mx(
                 out=wr[i][:, 256 * g0 : 256 * g1].bitcast(FP8X4), scales=wrs[i][:, 256 * g0 : 256 * g1],
-                in_=grp_r[:, g0:g1, :, :].rearrange("p g c t -> p (g c t)"),
+                in_=wstate[i][0][:, g0:g1, :, :].rearrange("p g c t -> p (g c t)"),
             )
+
+        def w_q_n(i, g0, g1):
             nc.vector.quantize_mx(
                 out=wn[i][:, 128 * g0 : 128 * g1].bitcast(FP8X4), scales=wns[i][:, 128 * g0 : 128 * g1],
-                in_=grp_n[:, g0:g1, :, :].rearrange("p g c t -> p (g c t)"),
+                in_=wstate[i][1][:, g0:g1, :, :].rearrange("p g c t -> p (g c t)"),
             )
 
-        hstate = {}
+        hgrp = {}
+        hcode = {}
 
-        def prep_h_alloc(q):
-            grp_h = stage.tile([P, 2, 2048], BF16, tag="grp_h", align_bytes=64)
-            hc = stage.tile([P, 2, 512], U32, tag="hc", align_bytes=64)
-            hs = stage.tile([P, 2, 512], U8, tag="hs", align_bytes=64)
-            hstate[q] = (grp_h, hc, hs)
-
-        def prep_h_part(q, g, jp):
-            grp_h, hc, hs = hstate[q]
+        def h_part(q, g, jp):
+            if (g, jp) == (0, 0):
+                grp_h = stage.tile([P, 2, 2048], BF16, tag="grp_h", align_bytes=64)
+                hgrp[q] = grp_h
+            grp_h = hgrp[q]
             words = hid[q][:].bitcast(F32)
             ht = ph.tile([P, 2, 2, P], F32, tag="h")
             for jj in range(2):
@@ -179,20 +182,32 @@ def tile_gptossmlaattention_pb_kernel(tc, hidden_states, cos, sin, Wq, bq, out_0
                 ),
                 in_=ht[:].rearrange("p jj u c -> p jj c u"),
             )
-            if jp == 1:
-                nc.vector.quantize_mx(out=hc[:, g, :].bitcast(FP8X4), scales=hs[:, g, :], in_=grp_h[:, g, :])
 
-        gstate = {}
+        def h_q(q, g):
+            if g == 0:
+                hc = stage.tile([P, 2, 512], U32, tag="hc", align_bytes=64)
+                hs = stage.tile([P, 2, 512], U8, tag="hs", align_bytes=64)
+                hcode[q] = (hc, hs)
+            hc, hs = hcode[q]
+            nc.vector.quantize_mx(out=hc[:, g, :].bitcast(FP8X4), scales=hs[:, g, :], in_=hgrp[q][:, g, :])
 
-        def mx_evac(n):
+        st_ms = {}
+        st_xt = {}
+        st_mn = {}
+        st_o = {}
+        st_tab = {}
+        st_rc = {}
+
+        def stage_a(n):
             q, i = divmod(n, NI)
-            grp_h, hc, hs = hstate[q]
+            hc, hs = hcode[q]
             ms = []
             for u in range(2):
                 m = pm.tile([P, 512], F32, tag="m")
                 ms.append(m)
-
-            def rope_pass(u, g):
+            st_ms[n] = ms
+            order = [(u, g) for g in range(2) for u in range(2)] if n == 0 else [(u, g) for u in range(2) for g in range(2)]
+            for u, g in order:
                 cols = slice(128 * u + 256 * g, 128 * u + 256 * g + 128)
                 nc.tensor.matmul_mx(
                     out=ms[u][:],
@@ -204,15 +219,19 @@ def tile_gptossmlaattention_pb_kernel(tc, hidden_states, cos, sin, Wq, bq, out_0
                     stop=(g == 1),
                 )
 
-            if n == 0:
-                for g in range(2):
-                    for u in range(2):
-                        rope_pass(u, g)
-            else:
-                for u in range(2):
-                    for g in range(2):
-                        rope_pass(u, g)
+        def stage_b(n, u):
+            q, i = divmod(n, NI)
+            xt = xpool.tile([P, 512], F32, tag="xt")
+            nc.scalar.activation(
+                out=xt[:], in_=st_ms[n][u][:], func=ACT.Identity, bias=bias[:, 2 * i + u : 2 * i + u + 1], scale=1.0
+            )
+            st_xt[(n, u)] = xt
+
+        def stage_c(n):
+            q, i = divmod(n, NI)
+            hc, hs = hcode[q]
             mn = pn.tile([P, 4, P], F32, tag="mn")
+            st_mn[n] = mn
             for j in range(4):
                 for g in range(2):
                     tok = slice(128 * j, 128 * (j + 1))
@@ -226,44 +245,48 @@ def tile_gptossmlaattention_pb_kernel(tc, hidden_states, cos, sin, Wq, bq, out_0
                         start=(g == 0),
                         stop=(g == 1),
                     )
-            xts = []
-            for u in range(2):
-                xt = xpool.tile([P, 512], F32, tag="xt")
-                nc.scalar.activation(
-                    out=xt[:], in_=ms[u][:], func=ACT.Identity, bias=bias[:, 2 * i + u : 2 * i + u + 1], scale=1.0
-                )
-                xts.append(xt)
+
+        def stage_ds(n):
             o = opool.tile([P, 2, 4, QK], F32, tag="o")
-            nc.scalar.copy(out=o[:, :, :, 0:NOPE], in_=mn[:].rearrange("p j (hh e) -> p hh j e", hh=2))
+            st_o[n] = o
+            nc.scalar.copy(out=o[:, :, :, 0:NOPE], in_=st_mn[n][:].rearrange("p j (hh e) -> p hh j e", hh=2))
+
+        def stage_dg(n):
+            q, i = divmod(n, NI)
+            o = st_o[n]
             nc.gpsimd.tensor_tensor(
                 out=o[:, :, :, 0:NOPE], in0=o[:, :, :, 0:NOPE],
                 in1=biasn[:, 2 * i : 2 * i + 2, :].unsqueeze(2).to_broadcast([P, 2, 4, NOPE]), op=ALU.add,
             )
-            gstate[n] = (xts, o)
 
-        def back_rope(n):
+        def stage_e(n, hh):
             q, i = divmod(n, NI)
-            xts, o = gstate[n]
-            tab = tmp.tile([P, 2, 2, 4, ROPE], F32, tag="tab")
-            for hh in range(2):
-                t = pt.tile([P, 4, P], F32, tag="t")
-                for j in range(4):
-                    nc.tensor.transpose(t[:, j, :], xts[hh][:, 128 * j : 128 * (j + 1)], ident[:])
-                nc.vector.tensor_tensor(
-                    out=tab[:, hh, :, :, :].rearrange("p c j d -> p c (j d)"),
-                    in0=t[:].rearrange("p j d -> p (j d)").unsqueeze(1).to_broadcast([P, 2, 512]),
-                    in1=cs[:, q, :, :, :].rearrange("p c j d -> p c (j d)"),
-                    op=ALU.mult,
-                )
-            last = n >= NG - 1
-            heads = ((0, 1), (1, 2)) if last else ((0, 2),)
-            for h0, h1 in heads:
+            if hh == 0:
+                tab = tmp.tile([P, 2, 2, 4, ROPE], F32, tag="tab")
+                st_tab[n] = tab
+            tab = st_tab[n]
+            t = pt.tile([P, 4, P], F32, tag="t")
+            for j in range(4):
+                nc.tensor.transpose(t[:, j, :], st_xt[(n, hh)][:, 128 * j : 128 * (j + 1)], ident[:])
+            nc.vector.tensor_tensor(
+                out=tab[:, :, hh, :, :].rearrange("p c j d -> p c (j d)"),
+                in0=t[:].rearrange("p j d -> p (j d)").unsqueeze(1).to_broadcast([P, 2, 512]),
+                in1=cs[:, q, :, :, :].rearrange("p c j d -> p c (j d)"),
+                op=ALU.mult,
+            )
+
+        def head_pieces(n):
+            return ((0, 1), (1, 2)) if n >= NG - 1 else ((0, 2),)
+
+        def stage_f(n):
+            q, i = divmod(n, NI)
+            o = st_o[n]
+            tab = st_tab[n]
+            for h0, h1 in head_pieces(n):
                 nc.gpsimd.tensor_tensor(
-                    out=o[:, h0:h1, :, NOPE : NOPE + 64], in0=tab[:, h0:h1, 0, :, 0:64], in1=tab[:, h0:h1, 1, :, 64:128],
-                    op=ALU.add,
-                )
-                nc.gpsimd.tensor_tensor(
-                    out=o[:, h0:h1, :, NOPE + 64 : QK], in0=tab[:, h0:h1, 0, :, 64:128], in1=tab[:, h0:h1, 1, :, 0:64],
+                    out=o[:, h0:h1, :, NOPE:QK].rearrange("p hh j (s e) -> p (hh j) s e", s=2),
+                    in0=tab[:, 0, h0:h1, :, :].rearrange("p hh j (s e) -> p (hh j) s e", s=2),
+                    in1=tab[:, 1, h0:h1, :, :].rearrange("p hh j (s e) -> p (hh j) s e", s=2)[:, :, ::-1, :],
                     op=ALU.add,
                 )
                 nc.sync.dma_start(
@@ -272,68 +295,141 @@ def tile_gptossmlaattention_pb_kernel(tc, hidden_states, cos, sin, Wq, bq, out_0
                     ),
                     in_=o[:, h0:h1, :, :].rearrange("p hh j e -> p hh (j e)"),
                 )
-            gstate[n] = o
 
-        def fin(n):
-            q, i = divmod(n, NI)
-            o = gstate[n]
-            am = tmp.tile([P, 8], F32, tag="am")
-            rc = tmp.tile([P, 8], F32, tag="rc")
-            r4 = tmp.tile([P, 8], F32, tag="r4")
-            last = n >= NG - 1
-            pieces = ((0, 4), (4, 8)) if last else ((0, 8),)
-            for k0, k1 in pieces:
+        st_am = {}
+        st_r4 = {}
+
+        def stage_max(n):
+            o = st_o[n]
+            am = stat.tile([P, 8], F32, tag="am")
+            st_am[n] = am
+            for h0, h1 in head_pieces(n):
+                k0, k1 = 4 * h0, 4 * h1
                 nc.vector.tensor_reduce(
                     out=am[:, k0:k1], in_=o[:].rearrange("p hh j e -> p (hh j) e")[:, k0:k1, :], axis=AX.X, op=ALU.max,
                     apply_absolute_value=True,
                 )
-                nc.vector.reciprocal(out=rc[:, k0:k1], in_=am[:, k0:k1])
-                nc.scalar.activation(out=r4[:, k0:k1], in_=rc[:, k0:k1], func=ACT.Copy, scale=448.0)
-            f8 = opool.tile([P, 2, 4, QK], FP8, tag="f8")
-            for hh in range(2):
-                for j in range(4):
-                    k = 4 * hh + j
-                    if n >= NG - 2 and j >= 2:
-                        nc.vector.tensor_scalar(
-                            out=f8[:, hh, j, :], in0=o[:, hh, j, :], scalar1=r4[:, k : k + 1], scalar2=None,
-                            op0=ALU.mult, saturate=False,
-                        )
-                    else:
-                        nc.scalar.activation(
-                            out=f8[:, hh, j, :], in_=o[:, hh, j, :], func=ACT.Identity,
-                            scale=r4[:, k : k + 1], bias=zero[:, 0:1], saturate=False,
-                        )
-                nc.sync.dma_start(
-                    out=out_1[0, 2 * i + hh, 512 * q : 512 * (q + 1), :].rearrange("(p j) e -> p (j e)", j=4),
-                    in_=f8[:, hh, :, :].rearrange("p j e -> p (j e)").bitcast(U8),
-                )
+                if n == NG - 1:
+                    stage_rc(n, k0, k1)
 
-        prep_h_alloc(0)
-        for g in range(2):
-            prep_w_copy(0, g, "v")
-            prep_h_part(0, g, 0)
-            prep_w_quant(0, g, g + 1)
-            prep_h_part(0, g, 1)
-        build_sinw(0, 1)
-        prep_w_copy(1, 0, "s")
-        prep_w_copy(1, 1, "s")
-        prep_w_quant(1, 0, 2)
-        for n in range(NG + 2):
+        def stage_rc(n, k0, k1):
+            if k0 == 0:
+                rc = stat.tile([P, 8], F32, tag="rc")
+                st_rc[n] = rc
+            nc.vector.reciprocal(out=st_rc[n][:, k0:k1], in_=st_am[n][:, k0:k1])
+
+        def stage_r4(n, k0, k1):
+            if k0 == 0:
+                r4 = stat.tile([P, 8], F32, tag="r4")
+                st_r4[n] = r4
+            nc.scalar.activation(out=st_r4[n][:, k0:k1], in_=st_rc[n][:, k0:k1], func=ACT.Copy, scale=448.0)
+
+        def stage_cast(n):
             q, i = divmod(n, NI)
-            if n < NG:
-                mx_evac(n)
-                if q == 0 and 1 <= i + 1 < NI - 1:
-                    prep_w_copy(i + 2, 0, "sg"[i])
-                    prep_w_copy(i + 2, 1, "sg"[i])
-                    prep_w_quant(i + 2, 0, 2)
-                if n == 1:
-                    build_sinw(1, NQ)
-                if q + 1 < NQ and i < 2:
-                    if i == 0:
-                        prep_h_alloc(q + 1)
-                    prep_h_part(q + 1, i, 0)
-                    prep_h_part(q + 1, i, 1)
-            if 0 <= n - 1 < NG:
-                back_rope(n - 1)
-            if 0 <= n - 2 < NG:
-                fin(n - 2)
+            o = st_o[n]
+            f8 = opool.tile([P, 2, 4, QK], FP8, tag="f8")
+            for h0, h1 in head_pieces(n):
+                if n == NG - 1:
+                    stage_r4(n, 4 * h0, 4 * h1)
+                r4 = st_r4[n]
+                for hh in range(h0, h1):
+                    for j in range(4):
+                        k = 4 * hh + j
+                        if n >= NG - 2 and j >= 2:
+                            nc.vector.tensor_scalar(
+                                out=f8[:, hh, j, :], in0=o[:, hh, j, :], scalar1=r4[:, k : k + 1], scalar2=None,
+                                op0=ALU.mult, saturate=False,
+                            )
+                        else:
+                            nc.scalar.activation(
+                                out=f8[:, hh, j, :], in_=o[:, hh, j, :], func=ACT.Identity,
+                                scale=r4[:, k : k + 1], bias=zero[:, 0:1], saturate=False,
+                            )
+                    nc.sync.dma_start(
+                        out=out_1[0, 2 * i + hh, 512 * q : 512 * (q + 1), :].rearrange("(p j) e -> p (j e)", j=4),
+                        in_=f8[:, hh, :, :].rearrange("p j e -> p (j e)").bitcast(U8),
+                    )
+
+        w_alloc(0)
+        h_part(0, 0, 0)
+        h_part(0, 0, 1)
+        w_il_r(0, 0, "v")
+        w_il_n(0, 0, "v")
+        w_q_r(0, 0, 1)
+        h_q(0, 0)
+        h_part(0, 1, 0)
+        h_part(0, 1, 1)
+        bt = pt.tile([P, 1024], BF16, tag="t")
+        nc.tensor.transpose(bt[:, 0:P], brow[:], identb[:])
+        nc.scalar.copy(out=bias[:], in_=bt[:, 0:8])
+        bn_ps = pt.tile([P, 512], F32, tag="t")
+        nc.tensor.matmul(out=bn_ps[:], lhsT=ones[:], rhs=bnrow[:], start=True, stop=True)
+        nc.scalar.copy(out=biasn[:].rearrange("p h e -> p (h e)"), in_=bn_ps[:])
+        w_il_r(0, 1, "v")
+        w_q_n(0, 0, 1)
+        w_q_r(0, 1, 2)
+        h_q(0, 1)
+        build_sinw(0, 1, 0)
+        build_sinw(0, 1, 1)
+        w_alloc(1)
+        w_il_n(1, 0, "s")
+        w_il_n(1, 1, "s")
+        w_il_n(0, 1, "v")
+        w_q_n(0, 1, 2)
+        w_il_r(1, 0, "v")
+        w_il_r(1, 1, "v")
+        w_q_n(1, 0, 2)
+        w_q_r(1, 0, 2)
+        w_alloc(2)
+        for g in range(2):
+            w_il_r(2, g, "g")
+            w_il_n(2, g, "g")
+
+        for s in range(NG + CAST_LAG + 1):
+            if s < NG:
+                stage_a(s)
+                stage_b(s, 0)
+            if 0 <= s - CAST_LAG < NG - 1:
+                stage_r4(s - CAST_LAG, 0, 8)
+            if s < NG:
+                stage_b(s, 1)
+                stage_c(s)
+            if 0 <= s - 1 < NG:
+                stage_f(s - 1)
+            if s < NG:
+                stage_ds(s)
+                stage_dg(s)
+                stage_e(s, 0)
+            if 0 <= s - 2 < NG - 1:
+                stage_rc(s - 2, 0, 8)
+            if s < NG:
+                stage_e(s, 1)
+            if s == 0:
+                w_q_r(2, 0, 2)
+                w_q_n(2, 0, 2)
+                w_alloc(3)
+                w_il_r(3, 0, "s")
+                w_il_n(3, 0, "s")
+            if s == 1:
+                w_il_r(3, 1, "s")
+                w_il_n(3, 1, "s")
+                w_q_r(3, 0, 2)
+                w_q_n(3, 0, 2)
+            if 0 <= s - 1 < NG:
+                stage_max(s - 1)
+            if 0 <= s - CAST_LAG < NG:
+                stage_cast(s - CAST_LAG)
+            if s == 1:
+                build_sinw(1, NQ, 0)
+            if s == 2:
+                build_sinw(1, NQ, 1)
+            if s == 1 or s == 2:
+                h_part(1, s - 1, 0)
+                h_part(1, s - 1, 1)
+                h_q(1, s - 1)
+            if 3 <= s < 11:
+                k = s - 3
+                qn, part = 2 + k // 4, k % 4
+                h_part(qn, part // 2, part % 2)
+                if part % 2 == 1:
+                    h_q(qn, part // 2)

@@ -22,7 +22,7 @@ NQ = 4
 NI = 4
 NG = NQ * NI
 CAST_LAG = 3
-N_WARM = 5
+N_WARM = 3
 
 
 def tile_gptossmlaattention_pb_kernel(tc, hidden_states, cos, sin, Wq, bq, out_0, out_1):
@@ -118,13 +118,18 @@ def tile_gptossmlaattention_pb_kernel(tc, hidden_states, cos, sin, Wq, bq, out_0
         for rep_i in range(N_WARM):
             nc.tensor.matmul(out=wps[:], lhsT=warm[:, 0:P], rhs=warm[:], start=True, stop=True)
 
-        def build_sinw(q0, q1, half):
+        def build_sinw(q0, q1, half, eng_name):
             lo, hi, sign = ((0, 64, 1.0), (64, 0, -1.0))[half]
-            nc.gpsimd.tensor_scalar(
-                out=cs[:, q0:q1, 1, :, lo : lo + 64],
-                in0=sinr[:, q0:q1, :, hi : hi + 64],
-                scalar1=sign, scalar2=0.0, op0=ALU.mult, op1=ALU.add,
-            )
+            if eng_name == "g":
+                nc.gpsimd.tensor_scalar(
+                    out=cs[:, q0:q1, 1, :, lo : lo + 64],
+                    in0=sinr[:, q0:q1, :, hi : hi + 64],
+                    scalar1=sign, scalar2=0.0, op0=ALU.mult, op1=ALU.add,
+                )
+            else:
+                nc.scalar.activation(
+                    out=cs[:, q0:q1, 1, :, lo : lo + 64], in_=sinr[:, q0:q1, :, hi : hi + 64], func=ACT.Copy, scale=sign
+                )
 
         def interleave(eng_name, out, in_):
             if eng_name == "v":
@@ -354,7 +359,7 @@ def tile_gptossmlaattention_pb_kernel(tc, hidden_states, cos, sin, Wq, bq, out_0
         h_part(0, 0, 0)
         h_part(0, 0, 1)
         w_il_r(0, 0, "v")
-        w_il_n(0, 0, "v")
+        w_il_n(0, 0, "s")
         w_q_r(0, 0, 1)
         h_q(0, 0)
         h_part(0, 1, 0)
@@ -369,12 +374,12 @@ def tile_gptossmlaattention_pb_kernel(tc, hidden_states, cos, sin, Wq, bq, out_0
         w_q_n(0, 0, 1)
         w_q_r(0, 1, 2)
         h_q(0, 1)
-        build_sinw(0, 1, 0)
-        build_sinw(0, 1, 1)
+        build_sinw(0, 1, 0, "g")
+        build_sinw(0, 1, 1, "g")
         w_alloc(1)
+        w_il_n(0, 1, "s")
         w_il_n(1, 0, "s")
         w_il_n(1, 1, "s")
-        w_il_n(0, 1, "v")
         w_q_n(0, 1, 2)
         w_il_r(1, 0, "v")
         w_il_r(1, 1, "v")
@@ -420,9 +425,9 @@ def tile_gptossmlaattention_pb_kernel(tc, hidden_states, cos, sin, Wq, bq, out_0
             if 0 <= s - CAST_LAG < NG:
                 stage_cast(s - CAST_LAG)
             if s == 1:
-                build_sinw(1, NQ, 0)
+                build_sinw(1, NQ, 0, "s")
             if s == 2:
-                build_sinw(1, NQ, 1)
+                build_sinw(1, NQ, 1, "s")
             if s == 1 or s == 2:
                 h_part(1, s - 1, 0)
                 h_part(1, s - 1, 1)

@@ -170,17 +170,27 @@ def tile_gptossmlaattention_pb_kernel(tc, hidden_states, cos, sin, Wq, bq, out_0
         hcode = {}
 
         def h_part(q, g, jp):
-            if (g, jp) == (0, 0):
-                grp_h = stage.tile([P, 2, 2048], BF16, tag="grp_h", align_bytes=64)
-                hgrp[q] = grp_h
-            grp_h = hgrp[q]
+            h_tr(q, g, jp)
+            h_cp(q, g, jp)
+
+        hts = {}
+
+        def h_tr(q, g, jp):
             words = hid[q][:].bitcast(F32)
             ht = ph.tile([P, 2, 2, P], F32, tag="h")
+            hts[(q, g, jp)] = ht
             for jj in range(2):
                 for u in range(2):
                     nc.tensor.transpose(
                         ht[:, jj, u, :], words[:, 2 * jp + jj, 256 * g + u : 256 * (g + 1) : 2], ident[:]
                     )
+
+        def h_cp(q, g, jp):
+            if (g, jp) == (0, 0):
+                grp_h = stage.tile([P, 2, 2048], BF16, tag="grp_h", align_bytes=64)
+                hgrp[q] = grp_h
+            grp_h = hgrp[q]
+            ht = hts[(q, g, jp)]
             nc.scalar.copy(
                 out=grp_h[:].bitcast(F32)[:, g, 512 * jp : 512 * (jp + 1)].rearrange(
                     "p (jj c u) -> p jj c u", jj=2, u=2
@@ -398,12 +408,18 @@ def tile_gptossmlaattention_pb_kernel(tc, hidden_states, cos, sin, Wq, bq, out_0
                 stage_r4(s - CAST_LAG, 0, 8)
             if s < NG:
                 stage_b(s, 1)
+            if s < NG:
                 stage_c(s)
+            if 3 <= s < 11:
+                h_tr(2 + (s - 3) // 4, ((s - 3) % 4) // 2, (s - 3) % 2)
             if 0 <= s - 1 < NG:
                 stage_f(s - 1)
             if s < NG:
                 stage_ds(s)
                 stage_dg(s)
+            if 3 <= s < 11:
+                h_cp(2 + (s - 3) // 4, ((s - 3) % 4) // 2, (s - 3) % 2)
+            if s < NG:
                 stage_e(s, 0)
             if 0 <= s - 2 < NG - 1:
                 stage_rc(s - 2, 0, 8)
@@ -420,6 +436,8 @@ def tile_gptossmlaattention_pb_kernel(tc, hidden_states, cos, sin, Wq, bq, out_0
                 w_il_n(3, 1, "s")
                 w_q_r(3, 0, 2)
                 w_q_n(3, 0, 2)
+            if 3 <= s < 11 and (s - 3) % 2 == 1:
+                h_q(2 + (s - 3) // 4, ((s - 3) % 4) // 2)
             if 0 <= s - 1 < NG:
                 stage_max(s - 1)
             if 0 <= s - CAST_LAG < NG:
@@ -432,9 +450,3 @@ def tile_gptossmlaattention_pb_kernel(tc, hidden_states, cos, sin, Wq, bq, out_0
                 h_part(1, s - 1, 0)
                 h_part(1, s - 1, 1)
                 h_q(1, s - 1)
-            if 3 <= s < 11:
-                k = s - 3
-                qn, part = 2 + k // 4, k % 4
-                h_part(qn, part // 2, part % 2)
-                if part % 2 == 1:
-                    h_q(qn, part // 2)

@@ -95,12 +95,12 @@ def tile_gptossmlaattention_pb_kernel(tc, hidden_states, cos, sin, Wq, bq, out_0
         load_w(0, 0)
         load_hid(0, 512, 1024)
         load_w(0, 1)
+        load_w(2, 0)
+        load_w(2, 1)
         load_w(1, 0)
         load_w(1, 1)
         load_sin(0, 1)
         load_cos(0, 1)
-        load_w(2, 0)
-        load_w(2, 1)
         load_w(3, 0)
         load_w(3, 1)
         load_hid(1, 0, HID)
@@ -120,11 +120,11 @@ def tile_gptossmlaattention_pb_kernel(tc, hidden_states, cos, sin, Wq, bq, out_0
 
         def build_sinw(q0, q1, half, eng_name):
             lo, hi, sign = ((0, 64, 1.0), (64, 0, -1.0))[half]
-            if eng_name == "g":
-                nc.gpsimd.tensor_scalar(
+            if eng_name == "v":
+                nc.vector.tensor_scalar(
                     out=cs[:, q0:q1, 1, :, lo : lo + 64],
                     in0=sinr[:, q0:q1, :, hi : hi + 64],
-                    scalar1=sign, scalar2=0.0, op0=ALU.mult, op1=ALU.add,
+                    scalar1=sign, scalar2=None, op0=ALU.mult,
                 )
             else:
                 nc.scalar.activation(
@@ -185,18 +185,17 @@ def tile_gptossmlaattention_pb_kernel(tc, hidden_states, cos, sin, Wq, bq, out_0
                         ht[:, jj, u, :], words[:, 2 * jp + jj, 256 * g + u : 256 * (g + 1) : 2], ident[:]
                     )
 
-        def h_cp(q, g, jp):
+        def h_cp(q, g, jp, eng_name="s"):
             if (g, jp) == (0, 0):
                 grp_h = stage.tile([P, 2, 2048], BF16, tag="grp_h", align_bytes=64)
                 hgrp[q] = grp_h
             grp_h = hgrp[q]
             ht = hts[(q, g, jp)]
-            nc.scalar.copy(
-                out=grp_h[:].bitcast(F32)[:, g, 512 * jp : 512 * (jp + 1)].rearrange(
-                    "p (jj c u) -> p jj c u", jj=2, u=2
-                ),
-                in_=ht[:].rearrange("p jj u c -> p jj c u"),
-            )
+            dst = grp_h[:].bitcast(F32)[:, g, 512 * jp : 512 * (jp + 1)].rearrange("p (jj c u) -> p jj c u", jj=2, u=2)
+            if eng_name == "s":
+                nc.scalar.copy(out=dst, in_=ht[:].rearrange("p jj u c -> p jj c u"))
+            else:
+                nc.vector.tensor_copy(out=dst, in_=ht[:].rearrange("p jj u c -> p jj c u"))
 
         def h_q(q, g):
             if g == 0:
@@ -373,7 +372,7 @@ def tile_gptossmlaattention_pb_kernel(tc, hidden_states, cos, sin, Wq, bq, out_0
         w_q_r(0, 0, 1)
         h_q(0, 0)
         h_part(0, 1, 0)
-        h_part(0, 1, 1)
+        h_tr(0, 1, 1)
         bt = pt.tile([P, 1024], BF16, tag="t")
         nc.tensor.transpose(bt[:, 0:P], brow[:], identb[:])
         nc.scalar.copy(out=bias[:], in_=bt[:, 0:8])
@@ -381,11 +380,10 @@ def tile_gptossmlaattention_pb_kernel(tc, hidden_states, cos, sin, Wq, bq, out_0
         nc.tensor.matmul(out=bn_ps[:], lhsT=ones[:], rhs=bnrow[:], start=True, stop=True)
         nc.scalar.copy(out=biasn[:].rearrange("p h e -> p (h e)"), in_=bn_ps[:])
         w_il_r(0, 1, "v")
-        w_q_n(0, 0, 1)
+        h_cp(0, 1, 1, "v")
         w_q_r(0, 1, 2)
         h_q(0, 1)
-        build_sinw(0, 1, 0, "g")
-        build_sinw(0, 1, 1, "g")
+        w_q_n(0, 0, 1)
         w_alloc(1)
         w_il_n(0, 1, "s")
         w_il_n(1, 0, "s")
@@ -395,6 +393,8 @@ def tile_gptossmlaattention_pb_kernel(tc, hidden_states, cos, sin, Wq, bq, out_0
         w_il_r(1, 1, "v")
         w_q_n(1, 0, 2)
         w_q_r(1, 0, 2)
+        build_sinw(0, 1, 0, "v")
+        build_sinw(0, 1, 1, "v")
         w_alloc(2)
         for g in range(2):
             w_il_r(2, g, "g")

@@ -313,18 +313,14 @@ def tile_gptossmlaattention_pb_kernel(tc, hidden_states, cos, sin, Wq, bq, out_0
         st_am = {}
         st_r4 = {}
 
-        def stage_max(n):
-            o = st_o[n]
-            am = stat.tile([P, 8], F32, tag="am")
-            st_am[n] = am
-            for h0, h1 in head_pieces(n):
-                k0, k1 = 4 * h0, 4 * h1
-                nc.vector.tensor_reduce(
-                    out=am[:, k0:k1], in_=o[:].rearrange("p hh j e -> p (hh j) e")[:, k0:k1, :], axis=AX.X, op=ALU.max,
-                    apply_absolute_value=True,
-                )
-                if n == NG - 1:
-                    stage_rc(n, k0, k1)
+        def stage_max(n, k0=0, k1=8):
+            if k0 == 0:
+                am = stat.tile([P, 8], F32, tag="am")
+                st_am[n] = am
+            nc.vector.tensor_reduce(
+                out=st_am[n][:, k0:k1], in_=st_o[n][:].rearrange("p hh j e -> p (hh j) e")[:, k0:k1, :], axis=AX.X,
+                op=ALU.max, apply_absolute_value=True,
+            )
 
         def stage_rc(n, k0, k1):
             if k0 == 0:
@@ -338,31 +334,36 @@ def tile_gptossmlaattention_pb_kernel(tc, hidden_states, cos, sin, Wq, bq, out_0
                 st_r4[n] = r4
             nc.scalar.activation(out=st_r4[n][:, k0:k1], in_=st_rc[n][:, k0:k1], func=ACT.Copy, scale=448.0)
 
-        def stage_cast(n):
+        st_f8 = {}
+
+        def cast_row(n, hh, j, eng_name):
+            if n not in st_f8:
+                f8 = opool.tile([P, 2, 4, QK], FP8, tag="f8")
+                st_f8[n] = f8
+            k = 4 * hh + j
+            if eng_name == "v":
+                nc.vector.tensor_scalar(
+                    out=st_f8[n][:, hh, j, :], in0=st_o[n][:, hh, j, :], scalar1=st_r4[n][:, k : k + 1], scalar2=None,
+                    op0=ALU.mult, saturate=False,
+                )
+            else:
+                nc.scalar.activation(
+                    out=st_f8[n][:, hh, j, :], in_=st_o[n][:, hh, j, :], func=ACT.Identity,
+                    scale=st_r4[n][:, k : k + 1], bias=zero[:, 0:1], saturate=False,
+                )
+
+        def store_f8(n, hh):
             q, i = divmod(n, NI)
-            o = st_o[n]
-            f8 = opool.tile([P, 2, 4, QK], FP8, tag="f8")
-            for h0, h1 in head_pieces(n):
-                if n == NG - 1:
-                    stage_r4(n, 4 * h0, 4 * h1)
-                r4 = st_r4[n]
-                for hh in range(h0, h1):
-                    for j in range(4):
-                        k = 4 * hh + j
-                        if n >= NG - 2 and j >= 2:
-                            nc.vector.tensor_scalar(
-                                out=f8[:, hh, j, :], in0=o[:, hh, j, :], scalar1=r4[:, k : k + 1], scalar2=None,
-                                op0=ALU.mult, saturate=False,
-                            )
-                        else:
-                            nc.scalar.activation(
-                                out=f8[:, hh, j, :], in_=o[:, hh, j, :], func=ACT.Identity,
-                                scale=r4[:, k : k + 1], bias=zero[:, 0:1], saturate=False,
-                            )
-                    nc.sync.dma_start(
-                        out=out_1[0, 2 * i + hh, 512 * q : 512 * (q + 1), :].rearrange("(p j) e -> p (j e)", j=4),
-                        in_=f8[:, hh, :, :].rearrange("p j e -> p (j e)").bitcast(U8),
-                    )
+            nc.sync.dma_start(
+                out=out_1[0, 2 * i + hh, 512 * q : 512 * (q + 1), :].rearrange("(p j) e -> p (j e)", j=4),
+                in_=st_f8[n][:, hh, :, :].rearrange("p j e -> p (j e)").bitcast(U8),
+            )
+
+        def stage_cast(n):
+            for hh in range(2):
+                for j in range(4):
+                    cast_row(n, hh, j, "s")
+                store_f8(n, hh)
 
         w_alloc(0)
         h_part(0, 0, 0)
@@ -398,9 +399,11 @@ def tile_gptossmlaattention_pb_kernel(tc, hidden_states, cos, sin, Wq, bq, out_0
         w_alloc(2)
         for g in range(2):
             w_il_r(2, g, "g")
+        for g in range(2):
             w_il_n(2, g, "g")
+        w_q_r(2, 0, 2)
 
-        for s in range(NG + CAST_LAG + 1):
+        for s in range(NG):
             if s < NG:
                 stage_a(s)
                 stage_b(s, 0)
@@ -426,7 +429,6 @@ def tile_gptossmlaattention_pb_kernel(tc, hidden_states, cos, sin, Wq, bq, out_0
             if s < NG:
                 stage_e(s, 1)
             if s == 0:
-                w_q_r(2, 0, 2)
                 w_q_n(2, 0, 2)
                 w_alloc(3)
                 w_il_r(3, 0, "s")
@@ -450,3 +452,26 @@ def tile_gptossmlaattention_pb_kernel(tc, hidden_states, cos, sin, Wq, bq, out_0
                 h_part(1, s - 1, 0)
                 h_part(1, s - 1, 1)
                 h_q(1, s - 1)
+
+        la, lb = NG - 2, NG - 1
+        stage_r4(NG - 3, 0, 8)
+        stage_f(lb)
+        stage_rc(la, 0, 8)
+        stage_cast(NG - 3)
+        stage_r4(la, 0, 8)
+        for hh in range(2):
+            stage_max(lb, 4 * hh, 4 * hh + 4)
+            for j in range(4):
+                cast_row(la, hh, j, "v" if j >= 4 - 2 else "s")
+            store_f8(la, hh)
+            if hh == 1:
+                for j in range(4 - 3):
+                    cast_row(lb, 0, j, "s")
+            stage_rc(lb, 4 * hh, 4 * hh + 4)
+            stage_r4(lb, 4 * hh, 4 * hh + 4)
+        for j in range(4 - 3, 4):
+            cast_row(lb, 0, j, "v")
+        store_f8(lb, 0)
+        for j in range(4):
+            cast_row(lb, 1, j, "v" if j >= 4 - 3 else "s")
+        store_f8(lb, 1)

from contextlib import ExitStack

import concourse.mybir as mybir
from concourse.masks import make_identity

F32 = mybir.dt.float32
BF16 = mybir.dt.bfloat16
U32 = mybir.dt.uint32
U8 = mybir.dt.uint8
FP8X4 = mybir.dt.float8_e4m3fn_x4
FP8 = mybir.dt.float8_e4m3fn
ACT = mybir.ActivationFunctionType
ALU = mybir.AluOpType
AX = mybir.AxisListType

S, HID, NH, NOPE, ROPE = 2048, 1024, 8, 64, 128
QK = NOPE + ROPE
FLOPS = 2 * S * HID * NH * QK

P = 128
NQ = 4
NI = 4
NG = NQ * NI
CAST_LAG = 3
N_WARM = 3


def tile_gptossmlaattention_pb_kernel(tc, hidden_states, cos, sin, Wq, bq, out_0, out_1):
    nc = tc.nc
    with ExitStack() as ctx:
        keep = ctx.enter_context(tc.tile_pool(name="keep", bufs=1))
        stage = ctx.enter_context(tc.tile_pool(name="stage", bufs=2))
        wstage = ctx.enter_context(tc.tile_pool(name="wstage", bufs=4))
        xpool = ctx.enter_context(tc.tile_pool(name="xpool", bufs=4))
        tmp = ctx.enter_context(tc.tile_pool(name="tmp", bufs=3))
        stat = ctx.enter_context(tc.tile_pool(name="stat", bufs=5))
        opool = ctx.enter_context(tc.tile_pool(name="opool", bufs=6))
        pm = ctx.enter_context(tc.psum_pool(name="pm", bufs=3))
        pn = ctx.enter_context(tc.psum_pool(name="pn", bufs=1))
        pt = ctx.enter_context(tc.psum_pool(name="pt", bufs=2))
        ph = ctx.enter_context(tc.psum_pool(name="ph", bufs=2))
        ctx.enter_context(tc.manual_schedule())

        hid = [keep.tile([P, 4, HID], BF16, name="hid%d" % q) for q in range(NQ)]
        wraw = [keep.tile([P, 2, 4, 384], BF16, name="wraw%d" % i) for i in range(NI)]
        cs = keep.tile([P, NQ, 2, 4, ROPE], BF16, name="cs")
        sinr = keep.tile([P, NQ, 4, ROPE], BF16, name="sinr")
        brow = keep.tile([P, P], BF16, name="brow")
        bnrow = keep.tile([P, 512], BF16, name="bnrow")
        warm = keep.tile([P, 512], BF16, name="warm")
        ident = keep.tile([P, P], F32, name="ident")
        zero = keep.tile([P, 1], F32, name="zero")
        ones = keep.tile([P, P], BF16, name="ones")
        identb = keep.tile([P, P], BF16, name="identb")
        bias = keep.tile([P, 8], F32, name="bias")
        biasn = keep.tile([P, NH, NOPE], F32, name="biasn")
        wr = [keep.tile([P, 512], U32, name="wr%d" % i, align_bytes=64) for i in range(NI)]
        wrs = [keep.tile([P, 512], U8, name="wrs%d" % i, align_bytes=64) for i in range(NI)]
        wn = [keep.tile([P, 256], U32, name="wn%d" % i, align_bytes=64) for i in range(NI)]
        wns = [keep.tile([P, 256], U8, name="wns%d" % i, align_bytes=64) for i in range(NI)]

        def load_hid(q, k0, k1):
            nc.sync.dma_start(
                out=hid[q][:, :, k0:k1],
                in_=hidden_states[0, 512 * q : 512 * (q + 1), k0:k1].rearrange("(p j) k -> p j k", j=4),
            )

        def load_w(i, g):
            nc.sync.dma_start(
                out=wraw[i][:, g, :, :],
                in_=Wq[512 * g : 512 * (g + 1), 384 * i : 384 * (i + 1)].rearrange("(p t) c -> p t c", t=4),
            )

        def load_sin(q0, q1):
            nc.sync.dma_start(
                out=sinr[:, q0:q1, :, :].rearrange("p q j d -> p q (j d)"),
                in_=sin[0, 512 * q0 : 512 * q1, :].rearrange("(q p j) d -> p q (j d)", p=P, j=4),
            )

        def load_cos(q0, q1):
            nc.sync.dma_start(
                out=cs[:, q0:q1, 0, :, :].rearrange("p q j d -> p q (j d)"),
                in_=cos[0, 512 * q0 : 512 * q1, :].rearrange("(q p j) d -> p q (j d)", p=P, j=4),
            )

        nc.vector.memset(warm[:], 0.0)
        nc.vector.memset(brow[:], 0.0)
        nc.gpsimd.memset(bnrow[:], 0.0)
        nc.scalar.dma_start(out=brow[0:8, :], in_=bq.rearrange("(h e) -> h e", e=QK)[:, NOPE:QK])
        nc.scalar.dma_start(
            out=bnrow[0:1, :].rearrange("o (h e) -> o h e", e=NOPE),
            in_=bq.rearrange("(o h e) -> o h e", o=1, e=QK)[:, :, 0:NOPE],
        )
        load_hid(0, 0, 512)
        load_w(0, 0)
        load_hid(0, 512, 1024)
        load_w(0, 1)
        load_w(2, 0)
        load_w(2, 1)
        load_w(1, 0)
        load_w(1, 1)
        load_sin(0, 1)
        load_cos(0, 1)
        load_w(3, 0)
        load_w(3, 1)
        load_hid(1, 0, HID)
        load_sin(1, NQ)
        load_cos(1, NQ)
        load_hid(2, 0, HID)
        load_hid(3, 0, HID)

        make_identity(nc, ident[:])
        make_identity(nc, identb[:])
        nc.vector.memset(zero[:], 0.0)
        nc.gpsimd.memset(ones[:], 1.0)

        wps = pm.tile([P, 512], F32, tag="m")
        for rep_i in range(N_WARM):
            nc.tensor.matmul(out=wps[:], lhsT=warm[:, 0:P], rhs=warm[:], start=True, stop=True)

        def build_sinw(q0, q1, half, eng_name):
            lo, hi, sign = ((0, 64, 1.0), (64, 0, -1.0))[half]
            if eng_name == "v":
                nc.vector.tensor_scalar(
                    out=cs[:, q0:q1, 1, :, lo : lo + 64],
                    in0=sinr[:, q0:q1, :, hi : hi + 64],
                    scalar1=sign, scalar2=None, op0=ALU.mult,
                )
            else:
                nc.scalar.activation(
                    out=cs[:, q0:q1, 1, :, lo : lo + 64], in_=sinr[:, q0:q1, :, hi : hi + 64], func=ACT.Copy, scale=sign
                )

        def interleave(eng_name, out, in_):
            if eng_name == "v":
                nc.vector.tensor_copy(out=out, in_=in_)
            elif eng_name == "s":
                nc.scalar.copy(out=out, in_=in_)
            else:
                nc.gpsimd.tensor_scalar(out=out, in0=in_, scalar1=1.0, scalar2=0.0, op0=ALU.mult, op1=ALU.add)

        wstate = {}

        def w_alloc(i):
            grp_r = wstage.tile([P, 2, 256, 4], BF16, tag="grp_r", align_bytes=64)
            grp_n = wstage.tile([P, 2, 128, 4], BF16, tag="grp_n", align_bytes=64)
            wstate[i] = (grp_r, grp_n)

        def w_il_r(i, g, eng_name):
            src = wraw[i][:, g, :, :].rearrange("p t (hh e) -> p hh e t", hh=2)
            interleave(eng_name, wstate[i][0][:, g, :, :].rearrange("p (hh d) t -> p hh d t", hh=2), src[:, :, NOPE:QK, :])

        def w_il_n(i, g, eng_name):
            src = wraw[i][:, g, :, :].rearrange("p t (hh e) -> p hh e t", hh=2)
            interleave(eng_name, wstate[i][1][:, g, :, :].rearrange("p (hh e) t -> p hh e t", hh=2), src[:, :, 0:NOPE, :])

        def w_q_r(i, g0, g1):
            nc.vector.quantize_mx(
                out=wr[i][:, 256 * g0 : 256 * g1].bitcast(FP8X4), scales=wrs[i][:, 256 * g0 : 256 * g1],
                in_=wstate[i][0][:, g0:g1, :, :].rearrange("p g c t -> p (g c t)"),
            )

        def w_q_n(i, g0, g1):
            nc.vector.quantize_mx(
                out=wn[i][:, 128 * g0 : 128 * g1].bitcast(FP8X4), scales=wns[i][:, 128 * g0 : 128 * g1],
                in_=wstate[i][1][:, g0:g1, :, :].rearrange("p g c t -> p (g c t)"),
            )

        hgrp = {}
        hcode = {}

        def h_part(q, g, jp):
            h_tr(q, g, jp)
            h_cp(q, g, jp)

        hts = {}

        def h_tr(q, g, jp):
            words = hid[q][:].bitcast(F32)
            ht = ph.tile([P, 2, 2, P], F32, tag="h")
            hts[(q, g, jp)] = ht
            for jj in range(2):
                for u in range(2):
                    nc.tensor.transpose(
                        ht[:, jj, u, :], words[:, 2 * jp + jj, 256 * g + u : 256 * (g + 1) : 2], ident[:]
                    )

        def h_cp(q, g, jp, eng_name="s"):
            if (g, jp) == (0, 0):
                grp_h = stage.tile([P, 2, 2048], BF16, tag="grp_h", align_bytes=64)
                hgrp[q] = grp_h
            grp_h = hgrp[q]
            ht = hts[(q, g, jp)]
            dst = grp_h[:].bitcast(F32)[:, g, 512 * jp : 512 * (jp + 1)].rearrange("p (jj c u) -> p jj c u", jj=2, u=2)
            if eng_name == "s":
                nc.scalar.copy(out=dst, in_=ht[:].rearrange("p jj u c -> p jj c u"))
            else:
                nc.vector.tensor_copy(out=dst, in_=ht[:].rearrange("p jj u c -> p jj c u"))

        def h_q(q, g):
            if g == 0:
                hc = stage.tile([P, 2, 512], U32, tag="hc", align_bytes=64)
                hs = stage.tile([P, 2, 512], U8, tag="hs", align_bytes=64)
                hcode[q] = (hc, hs)
            hc, hs = hcode[q]
            nc.vector.quantize_mx(out=hc[:, g, :].bitcast(FP8X4), scales=hs[:, g, :], in_=hgrp[q][:, g, :])

        st_ms = {}
        st_xt = {}
        st_mn = {}
        st_o = {}
        st_tab = {}
        st_rc = {}

        def stage_a(n):
            q, i = divmod(n, NI)
            hc, hs = hcode[q]
            ms = []
            for u in range(2):
                m = pm.tile([P, 512], F32, tag="m")
                ms.append(m)
            st_ms[n] = ms
            order = [(u, g) for g in range(2) for u in range(2)] if n == 0 else [(u, g) for u in range(2) for g in range(2)]
            for u, g in order:
                cols = slice(128 * u + 256 * g, 128 * u + 256 * g + 128)
                nc.tensor.matmul_mx(
                    out=ms[u][:],
                    lhsT=wr[i][:, cols].bitcast(FP8X4),
                    lhsT_scale=wrs[i][:, cols],
                    rhs=hc[:, g, :].bitcast(FP8X4),
                    rhs_scale=hs[:, g, :],
                    start=(g == 0),
                    stop=(g == 1),
                )

        def stage_b(n, u):
            q, i = divmod(n, NI)
            xt = xpool.tile([P, 512], F32, tag="xt")
            nc.scalar.activation(
                out=xt[:], in_=st_ms[n][u][:], func=ACT.Identity, bias=bias[:, 2 * i + u : 2 * i + u + 1], scale=1.0
            )
            st_xt[(n, u)] = xt

        def stage_c(n):
            q, i = divmod(n, NI)
            hc, hs = hcode[q]
            mn = pn.tile([P, 4, P], F32, tag="mn")
            st_mn[n] = mn
            for j in range(4):
                for g in range(2):
                    tok = slice(128 * j, 128 * (j + 1))
                    cols = slice(128 * g, 128 * (g + 1))
                    nc.tensor.matmul_mx(
                        out=mn[:, j, :],
                        lhsT=hc[:, g, tok].bitcast(FP8X4),
                        lhsT_scale=hs[:, g, tok],
                        rhs=wn[i][:, cols].bitcast(FP8X4),
                        rhs_scale=wns[i][:, cols],
                        start=(g == 0),
                        stop=(g == 1),
                    )

        def stage_ds(n):
            o = opool.tile([P, 2, 4, QK], F32, tag="o")
            st_o[n] = o
            nc.scalar.copy(out=o[:, :, :, 0:NOPE], in_=st_mn[n][:].rearrange("p j (hh e) -> p hh j e", hh=2))

        def stage_dg(n):
            q, i = divmod(n, NI)
            o = st_o[n]
            nc.gpsimd.tensor_tensor(
                out=o[:, :, :, 0:NOPE], in0=o[:, :, :, 0:NOPE],
                in1=biasn[:, 2 * i : 2 * i + 2, :].unsqueeze(2).to_broadcast([P, 2, 4, NOPE]), op=ALU.add,
            )

        def stage_e(n, hh):
            q, i = divmod(n, NI)
            if hh == 0:
                tab = tmp.tile([P, 2, 2, 4, ROPE], F32, tag="tab")
                st_tab[n] = tab
            tab = st_tab[n]
            t = pt.tile([P, 4, P], F32, tag="t")
            for j in range(4):
                nc.tensor.transpose(t[:, j, :], st_xt[(n, hh)][:, 128 * j : 128 * (j + 1)], ident[:])
            nc.vector.tensor_tensor(
                out=tab[:, :, hh, :, :].rearrange("p c j d -> p c (j d)"),
                in0=t[:].rearrange("p j d -> p (j d)").unsqueeze(1).to_broadcast([P, 2, 512]),
                in1=cs[:, q, :, :, :].rearrange("p c j d -> p c (j d)"),
                op=ALU.mult,
            )

        def head_pieces(n):
            return ((0, 1), (1, 2)) if n >= NG - 1 else ((0, 2),)

        def stage_f(n):
            q, i = divmod(n, NI)
            o = st_o[n]
            tab = st_tab[n]
            for h0, h1 in head_pieces(n):
                nc.gpsimd.tensor_tensor(
                    out=o[:, h0:h1, :, NOPE:QK].rearrange("p hh j (s e) -> p (hh j) s e", s=2),
                    in0=tab[:, 0, h0:h1, :, :].rearrange("p hh j (s e) -> p (hh j) s e", s=2),
                    in1=tab[:, 1, h0:h1, :, :].rearrange("p hh j (s e) -> p (hh j) s e", s=2)[:, :, ::-1, :],
                    op=ALU.add,
                )
                nc.sync.dma_start(
                    out=out_0[0, 2 * i + h0 : 2 * i + h1, 512 * q : 512 * (q + 1), :].rearrange(
                        "h (p j) e -> p h (j e)", j=4
                    ),
                    in_=o[:, h0:h1, :, :].rearrange("p hh j e -> p hh (j e)"),
                )

        st_am = {}
        st_r4 = {}

        def stage_max(n, k0=0, k1=8):
            if k0 == 0:
                am = stat.tile([P, 8], F32, tag="am")
                st_am[n] = am
            nc.vector.tensor_reduce(
                out=st_am[n][:, k0:k1], in_=st_o[n][:].rearrange("p hh j e -> p (hh j) e")[:, k0:k1, :], axis=AX.X,
                op=ALU.max, apply_absolute_value=True,
            )

        def stage_rc(n, k0, k1):
            if k0 == 0:
                rc = stat.tile([P, 8], F32, tag="rc")
                st_rc[n] = rc
            nc.vector.reciprocal(out=st_rc[n][:, k0:k1], in_=st_am[n][:, k0:k1])

        def stage_r4(n, k0, k1):
            if k0 == 0:
                r4 = stat.tile([P, 8], F32, tag="r4")
                st_r4[n] = r4
            nc.scalar.activation(out=st_r4[n][:, k0:k1], in_=st_rc[n][:, k0:k1], func=ACT.Copy, scale=448.0)

        st_f8 = {}

        def cast_row(n, hh, j, eng_name):
            if n not in st_f8:
                f8 = opool.tile([P, 2, 4, QK], FP8, tag="f8")
                st_f8[n] = f8
            k = 4 * hh + j
            if eng_name == "v":
                nc.vector.tensor_scalar(
                    out=st_f8[n][:, hh, j, :], in0=st_o[n][:, hh, j, :], scalar1=st_r4[n][:, k : k + 1], scalar2=None,
                    op0=ALU.mult, saturate=False,
                )
            else:
                nc.scalar.activation(
                    out=st_f8[n][:, hh, j, :], in_=st_o[n][:, hh, j, :], func=ACT.Identity,
                    scale=st_r4[n][:, k : k + 1], bias=zero[:, 0:1], saturate=False,
                )

        def store_f8(n, hh):
            q, i = divmod(n, NI)
            nc.sync.dma_start(
                out=out_1[0, 2 * i + hh, 512 * q : 512 * (q + 1), :].rearrange("(p j) e -> p (j e)", j=4),
                in_=st_f8[n][:, hh, :, :].rearrange("p j e -> p (j e)").bitcast(U8),
            )

        def stage_cast(n):
            for hh in range(2):
                for j in range(4):
                    cast_row(n, hh, j, "s")
                store_f8(n, hh)

        w_alloc(0)
        h_part(0, 0, 0)
        h_part(0, 0, 1)
        w_il_r(0, 0, "v")
        w_il_n(0, 0, "s")
        w_q_r(0, 0, 1)
        h_q(0, 0)
        h_part(0, 1, 0)
        h_tr(0, 1, 1)
        bt = pt.tile([P, 1024], BF16, tag="t")
        nc.tensor.transpose(bt[:, 0:P], brow[:], identb[:])
        nc.scalar.copy(out=bias[:], in_=bt[:, 0:8])
        bn_ps = pt.tile([P, 512], F32, tag="t")
        nc.tensor.matmul(out=bn_ps[:], lhsT=ones[:], rhs=bnrow[:], start=True, stop=True)
        nc.scalar.copy(out=biasn[:].rearrange("p h e -> p (h e)"), in_=bn_ps[:])
        w_il_r(0, 1, "v")
        h_cp(0, 1, 1, "v")
        w_q_r(0, 1, 2)
        h_q(0, 1)
        w_q_n(0, 0, 1)
        w_alloc(1)
        w_il_n(0, 1, "s")
        w_il_n(1, 0, "s")
        w_il_n(1, 1, "s")
        w_q_n(0, 1, 2)
        w_il_r(1, 0, "v")
        w_il_r(1, 1, "v")
        w_q_n(1, 0, 2)
        w_q_r(1, 0, 2)
        build_sinw(0, 1, 0, "v")
        build_sinw(0, 1, 1, "v")
        w_alloc(2)
        for g in range(2):
            w_il_r(2, g, "g")
        for g in range(2):
            w_il_n(2, g, "g")
        w_q_r(2, 0, 2)

        for s in range(NG):
            if s < NG:
                stage_a(s)
                stage_b(s, 0)
            if 0 <= s - CAST_LAG < NG - 1:
                stage_r4(s - CAST_LAG, 0, 8)
            if s < NG:
                stage_b(s, 1)
            if s < NG:
                stage_c(s)
            if 3 <= s < 11:
                h_tr(2 + (s - 3) // 4, ((s - 3) % 4) // 2, (s - 3) % 2)
            if 0 <= s - 1 < NG:
                stage_f(s - 1)
            if s < NG:
                stage_ds(s)
                stage_dg(s)
            if 3 <= s < 11:
                h_cp(2 + (s - 3) // 4, ((s - 3) % 4) // 2, (s - 3) % 2)
            if s < NG:
                stage_e(s, 0)
            if 0 <= s - 2 < NG - 1:
                stage_rc(s - 2, 0, 8)
            if s < NG:
                stage_e(s, 1)
            if s == 0:
                w_q_n(2, 0, 2)
                w_alloc(3)
                w_il_r(3, 0, "s")
                w_il_n(3, 0, "s")
            if s == 1:
                w_il_r(3, 1, "s")
                w_il_n(3, 1, "s")
                w_q_r(3, 0, 2)
                w_q_n(3, 0, 2)
            if 3 <= s < 11 and (s - 3) % 2 == 1:
                h_q(2 + (s - 3) // 4, ((s - 3) % 4) // 2)
            if 0 <= s - 1 < NG:
                stage_max(s - 1)
            if 0 <= s - CAST_LAG < NG:
                stage_cast(s - CAST_LAG)
            if s == 1:
                build_sinw(1, NQ, 0, "s")
            if s == 2:
                build_sinw(1, NQ, 1, "s")
            if s == 1 or s == 2:
                h_part(1, s - 1, 0)
                h_part(1, s - 1, 1)
                h_q(1, s - 1)

        la, lb = NG - 2, NG - 1
        stage_r4(NG - 3, 0, 8)
        stage_f(lb)
        stage_rc(la, 0, 8)
        stage_cast(NG - 3)
        stage_r4(la, 0, 8)
        for hh in range(2):
            stage_max(lb, 4 * hh, 4 * hh + 4)
            for j in range(4):
                cast_row(la, hh, j, "v" if j >= 4 - 2 else "s")
            store_f8(la, hh)
            if hh == 1:
                for j in range(4 - 3):
                    cast_row(lb, 0, j, "s")
            stage_rc(lb, 4 * hh, 4 * hh + 4)
            stage_r4(lb, 4 * hh, 4 * hh + 4)
        for j in range(4 - 3, 4):
            cast_row(lb, 0, j, "v")
        store_f8(lb, 0)
        for j in range(4):
            cast_row(lb, 1, j, "v" if j >= 4 - 3 else "s")
        store_f8(lb, 1)
